import numpy as np
import ml_dtypes


def mxq(x, axis, fmt="e4m3"):
    dtype, down = {"e4m3": (ml_dtypes.float8_e4m3fn, 7), "e5m2": (ml_dtypes.float8_e5m2, 14)}[fmt]
    v = np.moveaxis(np.asarray(x, np.float32).astype(ml_dtypes.bfloat16).astype(np.float64), axis, -1)
    blocks = v.reshape(v.shape[:-1] + (-1, 32))
    amax = np.abs(blocks).max(-1, keepdims=True)
    byte = np.maximum(np.where(amax > 0, np.frexp(amax)[1] - 1 + 127, 0) - down, 1)
    scale = np.exp2(byte - 127.0)
    codes = (blocks / scale).astype(np.float32).astype(dtype).astype(np.float64)
    return np.moveaxis((codes * scale).reshape(v.shape), -1, axis)


WIDE = False


def mx_kscale(k):
    if not WIDE:
        return np.ones(k)
    levels = np.array([10, -10, 5, -5, 0])
    if k % 512:
        return np.exp2(np.random.permutation(np.resize(levels, k // 32))).repeat(32)
    a = np.empty((k // 512, 16))
    for p in range(k // 512):
        a[p, :8] = np.random.permutation(np.resize(levels, 8))
        for g in range(8):
            far = levels[np.abs(levels - a[p, g]) >= 10]
            a[p, g + 8] = far[np.random.randint(len(far))]
    return np.exp2(a.ravel()).repeat(32)


BF16 = ml_dtypes.bfloat16


def bf(x):
    return np.asarray(x, np.float32).astype(BF16)


def f64(x):
    return np.asarray(x).astype(np.float64)


E2M1 = np.array([0.0, 0.5, 1.0, 1.5, 2.0, 3.0, 4.0, 6.0, -0.0, -0.5, -1.0, -1.5, -2.0, -3.0, -4.0, -6.0])


def pack_weight(w, fmt):
    k, n = w.shape
    w = f64(bf(w)).reshape(k // 32, 32, n)
    amax = np.abs(w).max(1)
    if fmt == "e4m3":
        byte = np.frexp(amax)[1] - 1 + 127 - 7
    else:
        mant, ex = np.frexp(amax / 6.0)
        byte = np.where(mant > 0.5, ex, ex - 1) + 127
    byte = np.clip(np.where(amax > 0, byte, 1), 1, 254)
    scaled = (w * np.exp2(127.0 - byte)[:, None, :]).reshape(k, n).astype(np.float32)
    by_word = np.ascontiguousarray(scaled.reshape(k // 512, 128, 4, n).transpose(0, 1, 3, 2))
    if fmt == "e4m3":
        words = by_word.astype(ml_dtypes.float8_e4m3fn).view(np.uint8)
    else:
        c = by_word.astype(ml_dtypes.float4_e2m1fn).view(np.uint8) & 0xF
        words = c[..., 0::2] | (c[..., 1::2] << 4)
    return np.ascontiguousarray(words), np.ascontiguousarray(byte.astype(np.uint8).reshape(k // 512, 16, n))


def unpack_weight(words, scales, fmt):
    g, p, n, _ = words.shape
    if fmt == "e4m3":
        vals = np.ascontiguousarray(words).view(ml_dtypes.float8_e4m3fn).astype(np.float64)
    else:
        nib = np.empty((g, p, n, 4), np.uint8)
        nib[..., 0::2] = words & 0xF
        nib[..., 1::2] = words >> 4
        vals = E2M1[nib]
    vals = vals * np.repeat(np.exp2(scales.astype(np.float64) - 127.0), 8, axis=1)[..., None]
    return vals.transpose(0, 1, 3, 2).reshape(g * 512, n)


B, S, D, E = 2, 512, 512, 512
SC = 1.5


def draw0():
    s, t = mx_kscale(D), mx_kscale(E)
    rn = np.random.standard_normal
    qs = np.sqrt(SC / np.sqrt(2.0 * E))
    ws = qs / np.sqrt(2.0 * D)
    x_re = bf(rn((B, S, D)) * s)
    x_im = bf(rn((B, S, D)) * s)
    Wq_re_words, Wq_re_scales = pack_weight((rn((E, D)) * ws * t[:, None] / s).T, "e4m3")
    Wq_im_words, Wq_im_scales = pack_weight((rn((E, D)) * ws * t[:, None] / s).T, "e4m3")
    bq_re = bf(rn(E) * 0.5 * qs * t)
    bq_im = bf(rn(E) * 0.5 * qs * t)
    Wk_re_words, Wk_re_scales = pack_weight((rn((E, D)) * ws / t[:, None] / s).T, "e4m3")
    Wk_im_words, Wk_im_scales = pack_weight((rn((E, D)) * ws / t[:, None] / s).T, "e4m3")
    bk_re = bf(rn(E) * 0.5 * qs / t)
    bk_im = bf(rn(E) * 0.5 * qs / t)
    return {"x_re": x_re, "x_im": x_im,
            "Wq_re_words": Wq_re_words, "Wq_re_scales": Wq_re_scales,
            "Wq_im_words": Wq_im_words, "Wq_im_scales": Wq_im_scales,
            "bq_re": bq_re, "bq_im": bq_im,
            "Wk_re_words": Wk_re_words, "Wk_re_scales": Wk_re_scales,
            "Wk_im_words": Wk_im_words, "Wk_im_scales": Wk_im_scales,
            "bk_re": bk_re, "bk_im": bk_im}


def cproj(xr, xi, w_re_words, w_re_scales, w_im_words, w_im_scales, b_re, b_im):
    wr = unpack_weight(w_re_words, w_re_scales, "e4m3")
    wi = unpack_weight(w_im_words, w_im_scales, "e4m3")
    y_re = (xr @ wr) - (xi @ wi) + f64(b_re)
    y_im = (xr @ wi) + (xi @ wr) + f64(b_im)
    return y_re, y_im


def core(x_re, x_im, Wq_re_words, Wq_re_scales, Wq_im_words, Wq_im_scales, bq_re, bq_im,
              Wk_re_words, Wk_re_scales, Wk_im_words, Wk_im_scales, bk_re, bk_im):
    xr = mxq(f64(x_re), 2, "e4m3")
    xi = mxq(f64(x_im), 2, "e4m3")
    q_re, q_im = cproj(xr, xi, Wq_re_words, Wq_re_scales, Wq_im_words, Wq_im_scales, bq_re, bq_im)
    k_re, k_im = cproj(xr, xi, Wk_re_words, Wk_re_scales, Wk_im_words, Wk_im_scales, bk_re, bk_im)
    return ((mxq(q_re, 2, "e4m3") @ mxq(k_re, 2, "e4m3").transpose(0, 2, 1))
            + (mxq(q_im, 2, "e4m3") @ mxq(k_im, 2, "e4m3").transpose(0, 2, 1)))


def e4m3fn_bytes(y):
    return np.clip(np.asarray(y, np.float64), -448.0, 448.0).astype(np.float32).astype(ml_dtypes.float8_e4m3fn).view(np.uint8)


def e4m3fn_values(b):
    return np.asarray(b, np.uint8).view(ml_dtypes.float8_e4m3fn).astype(np.float64)


def setup_inputs():
    d = draw0()
    x0 = np.asarray(d['x_re']).astype(np.float64)
    s = (np.max(np.abs(x0), axis=(0, 1), keepdims=True) / 448.0).astype(np.float32)
    out = {}
    for k, v in d.items():
        if k == 'x_re':
            out['x_re_bytes'] = e4m3fn_bytes(x0 / s.astype(np.float64))
            out['x_re_scale'] = s
        else:
            out[k] = v
    return out


def reference(x_re_bytes, x_re_scale, x_im, Wq_re_words, Wq_re_scales, Wq_im_words, Wq_im_scales, bq_re, bq_im, Wk_re_words, Wk_re_scales, Wk_im_words, Wk_im_scales, bk_re, bk_im):
    return core(e4m3fn_values(x_re_bytes) * x_re_scale.astype(np.float64), x_im, Wq_re_words, Wq_re_scales, Wq_im_words, Wq_im_scales, bq_re, bq_im, Wk_re_words, Wk_re_scales, Wk_im_words, Wk_im_scales, bk_re, bk_im)

@@ -1,0 +1,393 @@
+from contextlib import ExitStack
+
+import concourse.mybir as mybir
+from concourse.masks import make_identity
+
+B, S, D, E = 2, 512, 512, 512
+P = 128
+J = 4
+
+F32 = mybir.dt.float32
+BF16 = mybir.dt.bfloat16
+U32 = mybir.dt.uint32
+I32 = mybir.dt.int32
+U8 = mybir.dt.uint8
+FP8 = mybir.dt.float8_e4m3fn
+FP8X4 = mybir.dt.float8_e4m3fn_x4
+ADD = mybir.AluOpType.add
+MULT = mybir.AluOpType.mult
+IDENT = mybir.ActivationFunctionType.Identity
+
+FLOPS = 8 * 2 * B * S * D * E + 2 * 2 * B * S * S * E
+
+
+def tile_teleportationattention_pa_w8_kernel(
+    tc, x_re_bytes, x_re_scale, x_im,
+    wq_re_words, wq_re_scales, wq_im_words, wq_im_scales, bq_re, bq_im,
+    wk_re_words, wk_re_scales, wk_im_words, wk_im_scales, bk_re, bk_im, out,
+):
+    nc = tc.nc
+    with ExitStack() as ctx:
+        keep = ctx.enter_context(tc.tile_pool(name="keep", bufs=1))
+        psum = ctx.enter_context(tc.psum_pool(name="psum", bufs=8))
+        ctx.enter_context(tc.manual_schedule())
+
+        def sb(shape, dtype, name):
+            return keep.tile(shape, dtype, name=name, align_bytes=64)
+
+        x8 = [sb([P, J, D], U8, "x8_%d" % b) for b in range(B)]
+        xrb = [sb([P, J, D], BF16, "xrb_%d" % b) for b in range(B)]
+        xib = [sb([P, J, D], BF16, "xib_%d" % b) for b in range(B)]
+        xg = {}
+        xc = {}
+        xs = {}
+        for b in range(B):
+            for v in ("r", "i", "n"):
+                xg[b, v] = sb([P, S, 4], BF16, "xg_%d%s" % (b, v))
+                xc[b, v] = sb([P, S], U32, "xc_%d%s" % (b, v))
+                xs[b, v] = sb([P, S], U8, "xs_%d%s" % (b, v))
+        scol = sb([P, 4], F32, "scol")
+        names = ("q_re", "q_im", "k_re", "k_im")
+        wraw = {}
+        wperm = {}
+        bias = {}
+        for n in names:
+            wraw[n] = sb([P, E], I32, "wraw_" + n)
+            wperm[n] = sb([P, E], I32, "wperm_" + n)
+            bias[n] = sb([P, 4], BF16, "bias_" + n)
+        sraw = {}
+        sperm = {}
+        for n in ("q", "k"):
+            sraw[n] = sb([P, E], U8, "sraw_" + n)
+            sperm[n] = sb([P, E], U8, "sperm_" + n)
+        yg = {}
+        yc = {}
+        ys = {}
+        yst = {}
+        for b in range(B):
+            for n in names:
+                yg[b, n] = sb([P, S, 4], BF16, "yg_%d%s" % (b, n))
+                yc[b, n] = sb([P, S], U32, "yc_%d%s" % (b, n))
+                ys[b, n] = sb([P, S], U8, "ys_%d%s" % (b, n))
+                yst[b, n] = sb([P, 4, S], BF16, "yst_%d%s" % (b, n))
+        ot = [sb([P, J, S], F32, "ot_%d" % b) for b in range(B)]
+        ident = sb([P, P], F32, "ident")
+        warm = sb([P, 16], F32, "warm")
+
+        words = {"q_re": wq_re_words, "q_im": wq_im_words, "k_re": wk_re_words, "k_im": wk_im_words}
+        wscales = {"q_re": wq_re_scales, "q_im": wq_im_scales, "k_re": wk_re_scales, "k_im": wk_im_scales}
+        biases = {"q_re": bq_re, "q_im": bq_im, "k_re": bk_re, "k_im": bk_im}
+
+        nc.vector.memset(sraw["q"][:].bitcast(I32), 0)
+        nc.vector.memset(sraw["k"][:].bitcast(I32), 0)
+        nc.vector.memset(warm[:], 0.0)
+
+        def load_words(n):
+            nc.sync.dma_start(out=wraw[n][:], in_=words[n][0].rearrange("p n t -> p (n t)").bitcast(I32))
+
+        def load_scales(n):
+            k = 4 if n[2:] == "im" else 0
+            for q in range(4):
+                nc.sync.dma_start(
+                    out=sraw[n[0]][32 * q + k : 32 * q + k + 4, :].bitcast(I32),
+                    in_=wscales[n][0, 4 * q : 4 * q + 4, :].bitcast(I32),
+                )
+
+        def load_x(b):
+            nc.sync.dma_start(out=x8[b][:], in_=x_re_bytes[b].rearrange("(p j) k -> p j k", j=J))
+
+        def load_xi(b, h):
+            nc.scalar.dma_start(
+                out=xib[b][:, 2 * h : 2 * h + 2, :],
+                in_=x_im[b].rearrange("(p j) k -> p j k", j=J)[:, 2 * h : 2 * h + 2, :],
+            )
+
+        def dma_xi(eng, b, h):
+            eng.dma_start(
+                out=xib[b][:, 2 * h : 2 * h + 2, :],
+                in_=x_im[b].rearrange("(p j) k -> p j k", j=J)[:, 2 * h : 2 * h + 2, :],
+            )
+
+        def load_bias(n):
+            nc.gpsimd.dma_start(out=bias[n][:], in_=biases[n].rearrange("(p t) -> p t", t=4))
+
+        nc.gpsimd.dma_start(out=scol[:], in_=x_re_scale.rearrange("a b (p t) -> p (a b t)", t=4))
+        make_identity(nc, ident[:])
+        load_bias("q_im")
+        load_bias("q_re")
+        load_bias("k_im")
+        load_bias("k_re")
+        load_x(0)
+        load_scales("q_re")
+        dma_xi(nc.sync, 0, 0)
+        dma_xi(nc.sync, 0, 1)
+        load_words("q_re")
+        load_words("q_im")
+        load_scales("q_im")
+        load_x(1)
+        dma_xi(nc.sync, 1, 0)
+        dma_xi(nc.sync, 1, 1)
+        load_words("k_im")
+        load_words("k_re")
+        load_scales("k_im")
+        load_scales("k_re")
+
+        nc.scalar.activation(out=warm[:], in_=warm[:], func=IDENT, bias=warm[:, 0:1], scale=1.0)
+
+        def permute_words(n, eng):
+            eng.tensor_copy(
+                out=wperm[n][:].rearrange("p (t m) -> p t m", t=4),
+                in_=wraw[n][:].rearrange("p (m t) -> p t m", t=4),
+            )
+
+        def permute_scales(n, eng):
+            eng.tensor_copy(
+                out=sperm[n][:].rearrange("p (t m) -> p t m", t=4),
+                in_=sraw[n][:].rearrange("p (m t) -> p t m", t=4),
+            )
+
+        def cast(b, j, eng):
+            src = x8[b][:, j, :].bitcast(FP8)
+            if eng == "v":
+                nc.vector.tensor_copy(out=xrb[b][:, j, :], in_=src)
+            else:
+                nc.scalar.copy(out=xrb[b][:, j, :], in_=src)
+
+        def transposes_r(b, j):
+            bank = psum.tile([P, 2, 128], F32, name="bank")
+            w = xrb[b][:, j, :].bitcast(F32)
+            for u in range(2):
+                nc.tensor.transpose(bank[:, u, :], w[:, u:256:2], ident[:])
+            return bank
+
+        def evac_r1(b, j, bank):
+            nc.vector.tensor_tensor(
+                out=xg[b, "r"][:, 128 * j : 128 * j + 128, :].rearrange("p c (u e) -> p c u e", e=2),
+                in0=bank[:].rearrange("p u c -> p (u c)").bitcast(BF16).rearrange("p (u c e) -> p c u e", u=2, e=2),
+                in1=scol[:].rearrange("p (u e) -> p u e", e=2).unsqueeze(1).to_broadcast([P, 128, 2, 2]),
+                op=MULT,
+            )
+
+        def transposes(src, h):
+            bank = psum.tile([P, 2, 256], F32, name="bank")
+            for jj in range(2):
+                w = src[:, 2 * h + jj, :].bitcast(F32)
+                for u in range(2):
+                    nc.tensor.transpose(bank[:, u, 128 * jj : 128 * jj + 128], w[:, u:256:2], ident[:])
+            return bank
+
+        def evac_r(b, h, bank):
+            nc.vector.tensor_tensor(
+                out=xg[b, "r"][:, 256 * h : 256 * h + 256, :].rearrange("p c (u e) -> p c u e", e=2),
+                in0=bank[:].rearrange("p u c -> p (u c)").bitcast(BF16).rearrange("p (u c e) -> p c u e", u=2, e=2),
+                in1=scol[:].rearrange("p (u e) -> p u e", e=2).unsqueeze(1).to_broadcast([P, 256, 2, 2]),
+                op=MULT,
+            )
+
+        def evac_i(b, h, bank, eng):
+            o = xg[b, "i"][:, 256 * h : 256 * h + 256, :].rearrange("p c t -> p (c t)").bitcast(F32).rearrange("p (c u) -> p c u", u=2)
+            i = bank[:].rearrange("p u c -> p c u")
+            if eng == "v":
+                nc.vector.tensor_copy(out=o, in_=i)
+            else:
+                nc.scalar.copy(out=o, in_=i)
+
+        def quant(codes, scales, grouped, c0, c1):
+            nc.vector.quantize_mx(
+                out=codes[:, c0:c1].bitcast(FP8X4),
+                scales=scales[:, c0:c1],
+                in_=grouped[:, c0:c1, :].rearrange("p c t -> p (c t)"),
+            )
+
+        def quant_x(b, v, c0, c1):
+            quant(xc[b, v], xs[b, v], xg[b, v], c0, c1)
+
+        def quant_y(b, n, c0, c1):
+            quant(yc[b, n], ys[b, n], yg[b, n], c0, c1)
+
+        def negate(b, c0, c1):
+            nc.vector.tensor_scalar(
+                out=xg[b, "n"][:, c0:c1, :].rearrange("p c t -> p (c t)"),
+                in0=xg[b, "i"][:, c0:c1, :].rearrange("p c t -> p (c t)"),
+                scalar1=-1.0, scalar2=None, op0=MULT,
+            )
+
+        def passes(n):
+            if n[2:] == "im":
+                return (("i", n[:2] + "re"), ("r", n[:2] + "im"))
+            return (("r", n[:2] + "re"), ("n", n[:2] + "im"))
+
+        def project(o, b, n, t, c0, c1):
+            for i, (v, w) in enumerate(passes(n)):
+                k = 4 if w[2:] == "im" else 0
+                nc.tensor.matmul_mx(
+                    out=o,
+                    lhsT=wperm[w][:, 128 * t : 128 * t + 128].bitcast(FP8X4),
+                    lhsT_scale=sperm[w[0]][k:128, 128 * t : 128 * t + 128],
+                    rhs=xc[b, v][:, c0:c1].bitcast(FP8X4),
+                    rhs_scale=xs[b, v][:, c0:c1],
+                    start=(i == 0),
+                    stop=(i == 1),
+                )
+
+        def mm_v(b, n, j):
+            bank = psum.tile([P, 4, 128], F32, name="bank")
+            for t in range(4):
+                project(bank[:, t, :], b, n, t, 128 * j, 128 * j + 128)
+            return bank
+
+        def evac_v(b, n, j, bank):
+            nc.vector.tensor_tensor(
+                out=yg[b, n][:, 128 * j : 128 * j + 128, :],
+                in0=bank[:].rearrange("p t c -> p c t"),
+                in1=bias[n][:].unsqueeze(1).to_broadcast([P, 128, 4]),
+                op=ADD,
+            )
+
+        def mm_s(b, n, t):
+            bank = psum.tile([P, S], F32, name="bank")
+            project(bank[:], b, n, t, 0, S)
+            return bank
+
+        def mm_s_half(b, n, h, tt):
+            bank = psum.tile([P, 2, 256], F32, name="bank")
+            for i in range(2):
+                project(bank[:, i, :], b, n, 2 * tt + i, 256 * h, 256 * h + 256)
+            return bank
+
+        def evac_s(b, n, t, c0, c1, src):
+            nc.scalar.activation(
+                out=yst[b, n][:, t, c0:c1], in_=src, func=IDENT, bias=bias[n][:, t : t + 1], scale=1.0
+            )
+
+        def interleave_s(b, n, c0, c1):
+            nc.scalar.copy(
+                out=yg[b, n][:, c0:c1, :],
+                in_=yst[b, n][:, :, c0:c1].rearrange("p t c -> p c t"),
+            )
+
+        def score(b, j):
+            bank = psum.tile([P, S], F32, name="bank")
+            for i, v in enumerate(("im", "re")):
+                nc.tensor.matmul_mx(
+                    out=bank[:],
+                    lhsT=yc[b, "q_" + v][:, 128 * j : 128 * j + 128].bitcast(FP8X4),
+                    lhsT_scale=ys[b, "q_" + v][:, 128 * j : 128 * j + 128],
+                    rhs=yc[b, "k_" + v][:].bitcast(FP8X4),
+                    rhs_scale=ys[b, "k_" + v][:],
+                    start=(i == 0),
+                    stop=(i == 1),
+                )
+            return bank
+
+        def evac_score(b, j, bank, eng):
+            o = ot[b][:, j, :].rearrange("p (c i) -> p c i", i=J)
+            i = bank[:].rearrange("p (i c) -> p c i", i=J)
+            if eng == "v":
+                nc.vector.tensor_copy(out=o, in_=i)
+            else:
+                nc.scalar.copy(out=o, in_=i)
+            nc.sync.dma_start(
+                out=out[b].rearrange("(p j) k -> p j k", j=J)[:, j, :], in_=ot[b][:, j, :]
+            )
+
+        cast(0, 0, "v")
+        cast(0, 1, "s")
+        cast(0, 2, "v")
+        cast(0, 3, "s")
+        tr = {}
+        ti = {}
+        for j in range(4):
+            tr[j] = transposes_r(0, j)
+        for h in range(2):
+            ti[0, h] = transposes(xib[0], h)
+        evac_r1(0, 0, tr[0])
+        evac_r1(0, 1, tr[1])
+        evac_i(0, 0, ti[0, 0], "s")
+        evac_i(0, 1, ti[0, 1], "s")
+        evac_r1(0, 2, tr[2])
+        quant_x(0, "r", 0, 256)
+        permute_words("q_re", nc.vector)
+        quant_x(0, "i", 0, 256)
+        permute_words("q_im", nc.vector)
+        permute_scales("q", nc.vector)
+        negate(0, 0, 256)
+
+        def half_s(b, n, h, tt):
+            bank = mm_s_half(b, n, h, tt)
+            for i in range(2):
+                evac_s(b, n, 2 * tt + i, 256 * h, 256 * h + 256, bank[:, i, :])
+
+        def tile_v(b, n, j):
+            evac_v(b, n, j, mm_v(b, n, j))
+
+        def tile_s(b, n, t):
+            bank = mm_s(b, n, t)
+            evac_s(b, n, t, 0, S, bank[:])
+
+        half_s(0, "q_im", 0, 0)
+        quant_x(0, "n", 0, 256)
+        half_s(0, "q_im", 0, 1)
+        evac_r1(0, 3, tr[3])
+        half_s(0, "q_re", 0, 0)
+        half_s(0, "q_re", 0, 1)
+        quant_x(0, "i", 256, 512)
+        negate(0, 256, 512)
+        quant_x(0, "r", 256, 512)
+        quant_x(0, "n", 256, 512)
+        for j in range(4):
+            cast(1, j, "v")
+        half_s(0, "q_im", 1, 0)
+        half_s(0, "q_im", 1, 1)
+        for h in range(2):
+            ti[1, h] = transposes(xib[1], h)
+        tr[4] = transposes(xrb[1], 0)
+        tr[5] = transposes(xrb[1], 1)
+        evac_i(1, 0, ti[1, 0], "s")
+        evac_i(1, 1, ti[1, 1], "s")
+        permute_words("k_im", nc.vector)
+        permute_words("k_re", nc.vector)
+        half_s(0, "q_re", 1, 0)
+        half_s(0, "q_re", 1, 1)
+        evac_r(1, 0, tr[4])
+        permute_scales("k", nc.vector)
+        quant_x(1, "i", 0, 512)
+        evac_r(1, 1, tr[5])
+        negate(1, 0, 512)
+        quant_x(1, "r", 0, 512)
+        interleave_s(0, "q_im", 0, 512)
+        for j in range(4):
+            tile_v(0, "k_re", j)
+            half_s(0, "k_im", j // 2, j % 2)
+            if j == 1:
+                quant_x(1, "n", 0, 512)
+        interleave_s(0, "q_re", 0, 512)
+        for j in range(4):
+            tile_v(1, "q_im", j)
+            tile_s(1, "k_im", j)
+            if j == 0:
+                interleave_s(0, "k_im", 0, 512)
+                quant_y(0, "q_im", 0, 512)
+            if j == 1:
+                quant_y(0, "k_re", 0, 512)
+            if j == 2:
+                quant_y(0, "q_re", 0, 512)
+            if j == 3:
+                quant_y(0, "k_im", 0, 512)
+            tile_v(1, "k_re", j)
+        interleave_s(1, "k_im", 0, 512)
+        for j in range(4):
+            tile_v(1, "q_re", j)
+            if j == 0:
+                quant_y(1, "q_im", 0, 512)
+            if j == 1:
+                quant_y(1, "k_re", 0, 512)
+            if j == 2:
+                quant_y(1, "k_im", 0, 512)
+            if j > 0:
+                quant_y(1, "q_re", 128 * j - 128, 128 * j)
+            evac_score(0, j, score(0, j), "s")
+        quant_y(1, "q_re", 384, 512)
+        for j in range(4):
+            bank = score(1, j)
+            evac_score(1, j, bank, "s" if j % 2 else "v")

@@ -73,11 +73,13 @@ def tile_teleportationattention_pa_w8_kernel(
         ot = [sb([P, J, S], F32, "ot_%d" % b) for b in range(B)]
         ident = sb([P, P], F32, "ident")
         warm = sb([P, 16], F32, "warm")
+        wz = sb([P, 512], BF16, "wz")
 
         words = {"q_re": wq_re_words, "q_im": wq_im_words, "k_re": wk_re_words, "k_im": wk_im_words}
         wscales = {"q_re": wq_re_scales, "q_im": wq_im_scales, "k_re": wk_re_scales, "k_im": wk_im_scales}
         biases = {"q_re": bq_re, "q_im": bq_im, "k_re": bk_re, "k_im": bk_im}
 
+        nc.vector.memset(wz[:], 0.0)
         nc.vector.memset(sraw["q"][:].bitcast(I32), 0)
         nc.vector.memset(sraw["k"][:].bitcast(I32), 0)
         nc.vector.memset(warm[:], 0.0)
@@ -131,6 +133,11 @@ def tile_teleportationattention_pa_w8_kernel(
         load_words("k_re")
         load_scales("k_im")
         load_scales("k_re")
+
+        def warm_up(n):
+            bank = psum.tile([P, 512], F32, name="bank")
+            for i in range(n):
+                nc.tensor.matmul(bank[:], lhsT=wz[:, 0:128], rhs=wz[:], start=True, stop=True)
 
         nc.scalar.activation(out=warm[:], in_=warm[:], func=IDENT, bias=warm[:, 0:1], scale=1.0)
 
@@ -262,8 +269,8 @@ def tile_teleportationattention_pa_w8_kernel(
 
         def interleave_s(b, n, c0, c1):
             nc.scalar.copy(
-                out=yg[b, n][:, c0:c1, :],
-                in_=yst[b, n][:, :, c0:c1].rearrange("p t c -> p c t"),
+                out=yg[b, n][:, c0:c1, :].rearrange("p (c i) t -> p c t i", i=4),
+                in_=yst[b, n][:, :, c0:c1].rearrange("p t (c i) -> p c t i", i=4),
             )
 
         def score(b, j):
@@ -295,6 +302,7 @@ def tile_teleportationattention_pa_w8_kernel(
         cast(0, 1, "s")
         cast(0, 2, "v")
         cast(0, 3, "s")
+        warm_up(5)
         tr = {}
         ti = {}
         for j in range(4):
@@ -312,6 +320,8 @@ def tile_teleportationattention_pa_w8_kernel(
         permute_words("q_im", nc.vector)
         permute_scales("q", nc.vector)
         negate(0, 0, 256)
+
+        warm_up(5)
 
         def half_s(b, n, h, tt):
             bank = mm_s_half(b, n, h, tt)

@@ -18,6 +18,8 @@ ADD = mybir.AluOpType.add
 MULT = mybir.AluOpType.mult
 IDENT = mybir.ActivationFunctionType.Identity
 
+TOKENS = ("(p j) k -> p j k", "(j p) k -> p j k")
+
 FLOPS = 8 * 2 * B * S * D * E + 2 * 2 * B * S * S * E
 
 
@@ -79,8 +81,8 @@ def tile_teleportationattention_pa_w8_kernel(
         wscales = {"q_re": wq_re_scales, "q_im": wq_im_scales, "k_re": wk_re_scales, "k_im": wk_im_scales}
         biases = {"q_re": bq_re, "q_im": bq_im, "k_re": bk_re, "k_im": bk_im}
 
-        nc.vector.memset(wz[:], 0.0)
         nc.vector.memset(sraw["q"][:].bitcast(I32), 0)
+        nc.vector.memset(wz[:], 0.0)
         nc.vector.memset(sraw["k"][:].bitcast(I32), 0)
         nc.vector.memset(warm[:], 0.0)
 
@@ -96,18 +98,18 @@ def tile_teleportationattention_pa_w8_kernel(
                 )
 
         def load_x(b):
-            nc.sync.dma_start(out=x8[b][:], in_=x_re_bytes[b].rearrange("(p j) k -> p j k", j=J))
+            nc.sync.dma_start(out=x8[b][:], in_=x_re_bytes[b].rearrange(TOKENS[b], j=J))
 
         def load_xi(b, h):
             nc.scalar.dma_start(
                 out=xib[b][:, 2 * h : 2 * h + 2, :],
-                in_=x_im[b].rearrange("(p j) k -> p j k", j=J)[:, 2 * h : 2 * h + 2, :],
+                in_=x_im[b].rearrange(TOKENS[b], j=J)[:, 2 * h : 2 * h + 2, :],
             )
 
         def dma_xi(eng, b, h):
             eng.dma_start(
                 out=xib[b][:, 2 * h : 2 * h + 2, :],
-                in_=x_im[b].rearrange("(p j) k -> p j k", j=J)[:, 2 * h : 2 * h + 2, :],
+                in_=x_im[b].rearrange(TOKENS[b], j=J)[:, 2 * h : 2 * h + 2, :],
             )
 
         def load_bias(n):
@@ -122,15 +124,15 @@ def tile_teleportationattention_pa_w8_kernel(
         load_x(0)
         load_scales("q_re")
         dma_xi(nc.sync, 0, 0)
-        dma_xi(nc.sync, 0, 1)
         load_words("q_re")
         load_words("q_im")
         load_scales("q_im")
+        dma_xi(nc.sync, 0, 1)
         load_x(1)
         dma_xi(nc.sync, 1, 0)
         dma_xi(nc.sync, 1, 1)
-        load_words("k_im")
         load_words("k_re")
+        load_words("k_im")
         load_scales("k_im")
         load_scales("k_re")
 
@@ -273,29 +275,54 @@ def tile_teleportationattention_pa_w8_kernel(
                 in_=yst[b, n][:, :, c0:c1].rearrange("p t (c i) -> p c t i", i=4),
             )
 
-        def score(b, j):
-            bank = psum.tile([P, S], F32, name="bank")
-            for i, v in enumerate(("im", "re")):
-                nc.tensor.matmul_mx(
-                    out=bank[:],
-                    lhsT=yc[b, "q_" + v][:, 128 * j : 128 * j + 128].bitcast(FP8X4),
-                    lhsT_scale=ys[b, "q_" + v][:, 128 * j : 128 * j + 128],
-                    rhs=yc[b, "k_" + v][:].bitcast(FP8X4),
-                    rhs_scale=ys[b, "k_" + v][:],
-                    start=(i == 0),
-                    stop=(i == 1),
+        def interleave_g(b, n, c0, c1):
+            for c in range(c0, c1, 128):
+                nc.gpsimd.tensor_scalar(
+                    out=yg[b, n][:, c : c + 128, :],
+                    in0=yst[b, n][:, :, c : c + 128].rearrange("p t c -> p c t"),
+                    scalar1=1.0, scalar2=0.0, op0=MULT, op1=ADD,
                 )
-            return bank
 
-        def evac_score(b, j, bank, eng):
-            o = ot[b][:, j, :].rearrange("p (c i) -> p c i", i=J)
-            i = bank[:].rearrange("p (i c) -> p c i", i=J)
-            if eng == "v":
-                nc.vector.tensor_copy(out=o, in_=i)
-            else:
-                nc.scalar.copy(out=o, in_=i)
-            nc.sync.dma_start(
-                out=out[b].rearrange("(p j) k -> p j k", j=J)[:, j, :], in_=ot[b][:, j, :]
+        def score(b, j, eng):
+            banks = 1 if len(eng) == 1 else 2
+            w = S // banks
+            for i in range(banks):
+                bank = psum.tile([P, w], F32, name="bank")
+                for k, v in enumerate(("im", "re")):
+                    nc.tensor.matmul_mx(
+                        out=bank[:],
+                        lhsT=yc[b, "q_" + v][:, 128 * j : 128 * j + 128].bitcast(FP8X4),
+                        lhsT_scale=ys[b, "q_" + v][:, 128 * j : 128 * j + 128],
+                        rhs=yc[b, "k_" + v][:, w * i : w * i + w].bitcast(FP8X4),
+                        rhs_scale=ys[b, "k_" + v][:, w * i : w * i + w],
+                        start=(k == 0),
+                        stop=(k == 1),
+                    )
+                if b == 0:
+                    o = ot[b][:, j, :].rearrange("p (c i) -> p c i", i=J)
+                    a = bank[:].rearrange("p (i c) -> p c i", i=J)
+                else:
+                    o = ot[b][:, j, w * i : w * i + w]
+                    a = bank[:]
+                if eng[i] == "v":
+                    nc.vector.tensor_copy(out=o, in_=a)
+                else:
+                    nc.scalar.copy(out=o, in_=a)
+                nc.sync.dma_start(
+                    out=out[b].rearrange(TOKENS[b], j=J)[:, j, w * i : w * i + w],
+                    in_=ot[b][:, j, w * i : w * i + w],
+                )
+
+        def interleave_v(b, n, c0, c1):
+            nc.vector.tensor_copy(
+                out=yg[b, n][:, c0:c1, :],
+                in_=yst[b, n][:, :, c0:c1].rearrange("p t c -> p c t"),
+            )
+
+        def cast_all(b):
+            nc.vector.tensor_copy(
+                out=xrb[b][:].rearrange("p j k -> p (j k)"),
+                in_=x8[b][:].rearrange("p j k -> p (j k)").bitcast(FP8),
             )
 
         cast(0, 0, "v")
@@ -307,21 +334,18 @@ def tile_teleportationattention_pa_w8_kernel(
         ti = {}
         for j in range(4):
             tr[j] = transposes_r(0, j)
-        for h in range(2):
-            ti[0, h] = transposes(xib[0], h)
+            if j == 1:
+                ti[0, 0] = transposes(xib[0], 0)
         evac_r1(0, 0, tr[0])
         evac_r1(0, 1, tr[1])
         evac_i(0, 0, ti[0, 0], "s")
-        evac_i(0, 1, ti[0, 1], "s")
-        evac_r1(0, 2, tr[2])
-        quant_x(0, "r", 0, 256)
         permute_words("q_re", nc.vector)
-        quant_x(0, "i", 0, 256)
+        quant_x(0, "r", 0, 256)
         permute_words("q_im", nc.vector)
+        quant_x(0, "i", 0, 256)
         permute_scales("q", nc.vector)
         negate(0, 0, 256)
-
-        warm_up(5)
+        warm_up(3)
 
         def half_s(b, n, h, tt):
             bank = mm_s_half(b, n, h, tt)
@@ -336,68 +360,71 @@ def tile_teleportationattention_pa_w8_kernel(
             evac_s(b, n, t, 0, S, bank[:])
 
         half_s(0, "q_im", 0, 0)
-        quant_x(0, "n", 0, 256)
         half_s(0, "q_im", 0, 1)
+        quant_x(0, "n", 0, 256)
+        evac_r1(0, 2, tr[2])
         evac_r1(0, 3, tr[3])
+        ti[0, 1] = transposes(xib[0], 1)
+        evac_i(0, 1, ti[0, 1], "s")
         half_s(0, "q_re", 0, 0)
         half_s(0, "q_re", 0, 1)
+        quant_x(0, "r", 256, 512)
         quant_x(0, "i", 256, 512)
         negate(0, 256, 512)
-        quant_x(0, "r", 256, 512)
+        cast_all(1)
         quant_x(0, "n", 256, 512)
-        for j in range(4):
-            cast(1, j, "v")
         half_s(0, "q_im", 1, 0)
         half_s(0, "q_im", 1, 1)
         for h in range(2):
             ti[1, h] = transposes(xib[1], h)
-        tr[4] = transposes(xrb[1], 0)
-        tr[5] = transposes(xrb[1], 1)
-        evac_i(1, 0, ti[1, 0], "s")
-        evac_i(1, 1, ti[1, 1], "s")
-        permute_words("k_im", nc.vector)
-        permute_words("k_re", nc.vector)
+            evac_i(1, h, ti[1, h], "s")
         half_s(0, "q_re", 1, 0)
         half_s(0, "q_re", 1, 1)
-        evac_r(1, 0, tr[4])
+        tr4 = transposes(xrb[1], 0)
+        tr5 = transposes(xrb[1], 1)
+        permute_words("k_re", nc.vector)
+        permute_words("k_im", nc.vector)
         permute_scales("k", nc.vector)
+        evac_r(1, 0, tr4)
+        evac_r(1, 1, tr5)
+        interleave_g(0, "q_im", 0, 512)
+        for j in range(4):
+            tile_s(0, "k_im", j)
         quant_x(1, "i", 0, 512)
-        evac_r(1, 1, tr[5])
         negate(1, 0, 512)
         quant_x(1, "r", 0, 512)
-        interleave_s(0, "q_im", 0, 512)
         for j in range(4):
-            tile_v(0, "k_re", j)
-            half_s(0, "k_im", j // 2, j % 2)
-            if j == 1:
-                quant_x(1, "n", 0, 512)
-        interleave_s(0, "q_re", 0, 512)
+            tile_s(0, "k_re", j)
+        quant_x(1, "n", 0, 512)
+        interleave_g(0, "k_im", 0, 512)
+        interleave_g(0, "k_re", 0, 512)
+        quant_y(0, "q_im", 0, 512)
         for j in range(4):
             tile_v(1, "q_im", j)
             tile_s(1, "k_im", j)
-            if j == 0:
-                interleave_s(0, "k_im", 0, 512)
-                quant_y(0, "q_im", 0, 512)
-            if j == 1:
-                quant_y(0, "k_re", 0, 512)
+            interleave_s(0, "q_re", 128 * j, 128 * j + 128)
             if j == 2:
-                quant_y(0, "q_re", 0, 512)
-            if j == 3:
                 quant_y(0, "k_im", 0, 512)
-            tile_v(1, "k_re", j)
-        interleave_s(1, "k_im", 0, 512)
+        quant_y(0, "k_re", 0, 512)
+        interleave_g(1, "k_im", 0, 512)
         for j in range(4):
+            if j == 0:
+                tile_s(1, "k_re", 0)
+            if j < 3:
+                tile_s(1, "k_re", j + 1)
+            if j == 3:
+                interleave_s(1, "k_re", 0, 256)
+                interleave_v(1, "k_re", 256, 512)
             tile_v(1, "q_re", j)
             if j == 0:
-                quant_y(1, "q_im", 0, 512)
+                quant_y(0, "q_re", 0, 512)
             if j == 1:
-                quant_y(1, "k_re", 0, 512)
+                quant_y(1, "q_im", 0, 512)
             if j == 2:
                 quant_y(1, "k_im", 0, 512)
-            if j > 0:
-                quant_y(1, "q_re", 128 * j - 128, 128 * j)
-            evac_score(0, j, score(0, j), "s")
-        quant_y(1, "q_re", 384, 512)
+        quant_y(1, "k_re", 0, 512)
+        quant_y(1, "q_re", 0, 512)
         for j in range(4):
-            bank = score(1, j)
-            evac_score(1, j, bank, "s" if j % 2 else "v")
+            score(0, j, "s")
+        for j in range(4):
+            score(1, j, ("v", "s", "v", "sv")[j])

@@ -16,11 +16,15 @@ FP8 = mybir.dt.float8_e4m3fn
 FP8X4 = mybir.dt.float8_e4m3fn_x4
 ADD = mybir.AluOpType.add
 MULT = mybir.AluOpType.mult
+COPY = mybir.ActivationFunctionType.Copy
 IDENT = mybir.ActivationFunctionType.Identity
 
 TOKENS = ("(p j) k -> p j k", "(j p) k -> p j k")
 
 FLOPS = 8 * 2 * B * S * D * E + 2 * 2 * B * S * S * E
+
+XSLOT = {"r": 0, "i": 1, "n": 2}
+HALVES = (1, 1)
 
 
 def tile_teleportationattention_pa_w8_kernel(
@@ -40,38 +44,34 @@ def tile_teleportationattention_pa_w8_kernel(
         x8 = [sb([P, J, D], U8, "x8_%d" % b) for b in range(B)]
         xrb = [sb([P, J, D], BF16, "xrb_%d" % b) for b in range(B)]
         xib = [sb([P, J, D], BF16, "xib_%d" % b) for b in range(B)]
-        xg = {}
-        xc = {}
-        xs = {}
-        for b in range(B):
-            for v in ("r", "i", "n"):
-                xg[b, v] = sb([P, S, 4], BF16, "xg_%d%s" % (b, v))
-                xc[b, v] = sb([P, S], U32, "xc_%d%s" % (b, v))
-                xs[b, v] = sb([P, S], U8, "xs_%d%s" % (b, v))
+        xg = [sb([P, HALVES[b], 3, S // HALVES[b], 4], BF16, "xg_%d" % b) for b in range(B)]
+        xc = [sb([P, HALVES[b], 3, S // HALVES[b]], U32, "xc_%d" % b) for b in range(B)]
+        xs = [sb([P, HALVES[b], 3, S // HALVES[b]], U8, "xs_%d" % b) for b in range(B)]
         scol = sb([P, 4], F32, "scol")
-        names = ("q_re", "q_im", "k_re", "k_im")
         wraw = {}
         wperm = {}
-        bias = {}
-        for n in names:
-            wraw[n] = sb([P, E], I32, "wraw_" + n)
-            wperm[n] = sb([P, E], I32, "wperm_" + n)
-            bias[n] = sb([P, 4], BF16, "bias_" + n)
         sraw = {}
         sperm = {}
         for n in ("q", "k"):
+            wraw[n] = sb([P, 2, E], I32, "wraw_" + n)
+            wperm[n] = sb([P, 2, E], I32, "wperm_" + n)
             sraw[n] = sb([P, E], U8, "sraw_" + n)
             sperm[n] = sb([P, E], U8, "sperm_" + n)
+        PART = {"im": 0, "re": 1}
+        bias = {}
+        for n in ("q_re", "q_im", "k_re", "k_im"):
+            bias[n] = sb([P, 4], BF16, "bias_" + n)
         yg = {}
         yc = {}
         ys = {}
-        yst = {}
         for b in range(B):
-            for n in names:
-                yg[b, n] = sb([P, S, 4], BF16, "yg_%d%s" % (b, n))
-                yc[b, n] = sb([P, S], U32, "yc_%d%s" % (b, n))
-                ys[b, n] = sb([P, S], U8, "ys_%d%s" % (b, n))
-                yst[b, n] = sb([P, 4, S], BF16, "yst_%d%s" % (b, n))
+            for n in ("q", "k"):
+                yg[b, n] = sb([P, 2, S, 4], BF16, "yg_%d%s" % (b, n))
+                yc[b, n] = sb([P, 2, S], U32, "yc_%d%s" % (b, n))
+                ys[b, n] = sb([P, 2, S], U8, "ys_%d%s" % (b, n))
+        yst = {}
+        for b, n in ((0, "q_im"), (0, "q_re"), (0, "k_im"), (1, "k_im")):
+            yst[b, n] = sb([P, 2, S, 2], BF16, "yst_%d%s" % (b, n))
         ot = [sb([P, J, S], F32, "ot_%d" % b) for b in range(B)]
         ident = sb([P, P], F32, "ident")
         warm = sb([P, 16], F32, "warm")
@@ -87,10 +87,10 @@ def tile_teleportationattention_pa_w8_kernel(
         nc.vector.memset(warm[:], 0.0)
 
         def load_words(n):
-            nc.sync.dma_start(out=wraw[n][:], in_=words[n][0].rearrange("p n t -> p (n t)").bitcast(I32))
+            nc.sync.dma_start(out=wraw[n[0]][:, PART[n[2:]], :], in_=words[n][0].rearrange("p n t -> p (n t)").bitcast(I32))
 
         def load_scales(n):
-            k = 4 if n[2:] == "im" else 0
+            k = 4 * PART[n[2:]]
             for q in range(4):
                 nc.sync.dma_start(
                     out=sraw[n[0]][32 * q + k : 32 * q + k + 4, :].bitcast(I32),
@@ -100,41 +100,32 @@ def tile_teleportationattention_pa_w8_kernel(
         def load_x(b):
             nc.sync.dma_start(out=x8[b][:], in_=x_re_bytes[b].rearrange(TOKENS[b], j=J))
 
-        def load_xi(b, h):
-            nc.scalar.dma_start(
-                out=xib[b][:, 2 * h : 2 * h + 2, :],
-                in_=x_im[b].rearrange(TOKENS[b], j=J)[:, 2 * h : 2 * h + 2, :],
-            )
-
-        def dma_xi(eng, b, h):
-            eng.dma_start(
-                out=xib[b][:, 2 * h : 2 * h + 2, :],
-                in_=x_im[b].rearrange(TOKENS[b], j=J)[:, 2 * h : 2 * h + 2, :],
-            )
+        def load_xi(eng, b, h0, h1):
+            eng.dma_start(out=xib[b][:, 2 * h0 : 2 * h1, :], in_=x_im[b].rearrange(TOKENS[b], j=J)[:, 2 * h0 : 2 * h1, :])
 
         def load_bias(n):
             nc.gpsimd.dma_start(out=bias[n][:], in_=biases[n].rearrange("(p t) -> p t", t=4))
 
         nc.gpsimd.dma_start(out=scol[:], in_=x_re_scale.rearrange("a b (p t) -> p (a b t)", t=4))
         make_identity(nc, ident[:])
-        load_bias("q_im")
-        load_bias("q_re")
-        load_bias("k_im")
-        load_bias("k_re")
         load_x(0)
         load_scales("q_re")
-        dma_xi(nc.sync, 0, 0)
+        load_x(1)
+        load_xi(nc.sync, 0, 0, 1)
+        load_xi(nc.sync, 0, 1, 2)
+        load_xi(nc.sync, 1, 0, 1)
         load_words("q_re")
         load_words("q_im")
         load_scales("q_im")
-        dma_xi(nc.sync, 0, 1)
-        load_x(1)
-        dma_xi(nc.sync, 1, 0)
-        dma_xi(nc.sync, 1, 1)
+        load_xi(nc.sync, 1, 1, 2)
+        load_bias("q_im")
+        load_bias("q_re")
+        load_bias("k_re")
+        load_bias("k_im")
         load_words("k_re")
         load_words("k_im")
-        load_scales("k_im")
         load_scales("k_re")
+        load_scales("k_im")
 
         def warm_up(n):
             bank = psum.tile([P, 512], F32, name="bank")
@@ -143,158 +134,132 @@ def tile_teleportationattention_pa_w8_kernel(
 
         nc.scalar.activation(out=warm[:], in_=warm[:], func=IDENT, bias=warm[:, 0:1], scale=1.0)
 
-        def permute_words(n, eng):
-            eng.tensor_copy(
-                out=wperm[n][:].rearrange("p (t m) -> p t m", t=4),
-                in_=wraw[n][:].rearrange("p (m t) -> p t m", t=4),
+        def permute_words(n, a, z):
+            nc.vector.tensor_copy(
+                out=wperm[n][:, a:z, :].rearrange("p w (t m) -> p w t m", t=4),
+                in_=wraw[n][:, a:z, :].rearrange("p w (m t) -> p w t m", t=4),
             )
 
-        def permute_scales(n, eng):
-            eng.tensor_copy(
+        def permute_scales(n):
+            nc.vector.tensor_copy(
                 out=sperm[n][:].rearrange("p (t m) -> p t m", t=4),
                 in_=sraw[n][:].rearrange("p (m t) -> p t m", t=4),
             )
 
-        def cast(b, j, eng):
-            src = x8[b][:, j, :].bitcast(FP8)
+        def cast(b, j0, j1, eng):
+            src = x8[b][:, j0:j1, :].bitcast(FP8)
             if eng == "v":
-                nc.vector.tensor_copy(out=xrb[b][:, j, :], in_=src)
+                nc.vector.tensor_copy(out=xrb[b][:, j0:j1, :], in_=src)
             else:
-                nc.scalar.copy(out=xrb[b][:, j, :], in_=src)
+                nc.scalar.copy(out=xrb[b][:, j0:j1, :], in_=src)
 
-        def transposes_r(b, j):
-            bank = psum.tile([P, 2, 128], F32, name="bank")
-            w = xrb[b][:, j, :].bitcast(F32)
-            for u in range(2):
-                nc.tensor.transpose(bank[:, u, :], w[:, u:256:2], ident[:])
-            return bank
+        def xpart(t, b, v, c0, c1):
+            n = S // HALVES[b]
+            h = c0 // n
+            return t[b][:, h, XSLOT[v], c0 - h * n : c1 - h * n]
 
-        def evac_r1(b, j, bank):
-            nc.vector.tensor_tensor(
-                out=xg[b, "r"][:, 128 * j : 128 * j + 128, :].rearrange("p c (u e) -> p c u e", e=2),
-                in0=bank[:].rearrange("p u c -> p (u c)").bitcast(BF16).rearrange("p (u c e) -> p c u e", u=2, e=2),
-                in1=scol[:].rearrange("p (u e) -> p u e", e=2).unsqueeze(1).to_broadcast([P, 128, 2, 2]),
-                op=MULT,
-            )
-
-        def transposes(src, h):
-            bank = psum.tile([P, 2, 256], F32, name="bank")
-            for jj in range(2):
-                w = src[:, 2 * h + jj, :].bitcast(F32)
+        def transposes(src, j0, n):
+            bank = psum.tile([P, 2, 128 * n], F32, name="bank")
+            for jj in range(n):
+                w = src[:, j0 + jj, :].bitcast(F32)
                 for u in range(2):
                     nc.tensor.transpose(bank[:, u, 128 * jj : 128 * jj + 128], w[:, u:256:2], ident[:])
             return bank
 
-        def evac_r(b, h, bank):
+        def evac_r(b, j0, n, bank):
             nc.vector.tensor_tensor(
-                out=xg[b, "r"][:, 256 * h : 256 * h + 256, :].rearrange("p c (u e) -> p c u e", e=2),
+                out=xpart(xg, b, "r", 128 * j0, 128 * (j0 + n)).rearrange("p c (u e) -> p c u e", e=2),
                 in0=bank[:].rearrange("p u c -> p (u c)").bitcast(BF16).rearrange("p (u c e) -> p c u e", u=2, e=2),
-                in1=scol[:].rearrange("p (u e) -> p u e", e=2).unsqueeze(1).to_broadcast([P, 256, 2, 2]),
+                in1=scol[:].rearrange("p (u e) -> p u e", e=2).unsqueeze(1).to_broadcast([P, 128 * n, 2, 2]),
                 op=MULT,
             )
 
-        def evac_i(b, h, bank, eng):
-            o = xg[b, "i"][:, 256 * h : 256 * h + 256, :].rearrange("p c t -> p (c t)").bitcast(F32).rearrange("p (c u) -> p c u", u=2)
-            i = bank[:].rearrange("p u c -> p c u")
+        def evac_i(b, j0, n, bank):
+            nc.scalar.copy(
+                out=xpart(xg, b, "i", 128 * j0, 128 * (j0 + n)).rearrange("p c t -> p (c t)").bitcast(F32).rearrange("p (c u) -> p c u", u=2),
+                in_=bank[:].rearrange("p u c -> p c u"),
+            )
+
+        def negate(b, c0, c1, eng):
+            o = xg[b][:, 0, 2, c0:c1].rearrange("p c t -> p (c t)")
+            i = xg[b][:, 0, 1, c0:c1].rearrange("p c t -> p (c t)")
             if eng == "v":
-                nc.vector.tensor_copy(out=o, in_=i)
+                nc.vector.tensor_scalar(out=o, in0=i, scalar1=-1.0, scalar2=None, op0=MULT)
             else:
-                nc.scalar.copy(out=o, in_=i)
+                nc.scalar.activation(out=o, in_=i, func=COPY, scale=-1.0)
 
-        def quant(codes, scales, grouped, c0, c1):
+        def quant_x(b, a, z, c0, c1):
+            assert z - a == 1 or c1 - c0 == S
             nc.vector.quantize_mx(
-                out=codes[:, c0:c1].bitcast(FP8X4),
-                scales=scales[:, c0:c1],
-                in_=grouped[:, c0:c1, :].rearrange("p c t -> p (c t)"),
+                out=xc[b][:, 0, a:z, c0:c1].rearrange("p v c -> p (v c)").bitcast(FP8X4),
+                scales=xs[b][:, 0, a:z, c0:c1].rearrange("p v c -> p (v c)"),
+                in_=xg[b][:, 0, a:z, c0:c1].rearrange("p v c t -> p (v c t)"),
             )
 
-        def quant_x(b, v, c0, c1):
-            quant(xc[b, v], xs[b, v], xg[b, v], c0, c1)
-
-        def quant_y(b, n, c0, c1):
-            quant(yc[b, n], ys[b, n], yg[b, n], c0, c1)
-
-        def negate(b, c0, c1):
-            nc.vector.tensor_scalar(
-                out=xg[b, "n"][:, c0:c1, :].rearrange("p c t -> p (c t)"),
-                in0=xg[b, "i"][:, c0:c1, :].rearrange("p c t -> p (c t)"),
-                scalar1=-1.0, scalar2=None, op0=MULT,
+        def quant_y(b, n, a, z, c0, c1):
+            nc.vector.quantize_mx(
+                out=yc[b, n][:, a:z, c0:c1].rearrange("p v c -> p (v c)").bitcast(FP8X4),
+                scales=ys[b, n][:, a:z, c0:c1].rearrange("p v c -> p (v c)"),
+                in_=yg[b, n][:, a:z, c0:c1, :].rearrange("p v c t -> p (v c t)"),
             )
-
-        def passes(n):
-            if n[2:] == "im":
-                return (("i", n[:2] + "re"), ("r", n[:2] + "im"))
-            return (("r", n[:2] + "re"), ("n", n[:2] + "im"))
 
         def project(o, b, n, t, c0, c1):
-            for i, (v, w) in enumerate(passes(n)):
-                k = 4 if w[2:] == "im" else 0
+            for i, (v, w) in enumerate(((("i", "re"), ("r", "im")) if n[2:] == "im" else (("r", "re"), ("n", "im")))):
                 nc.tensor.matmul_mx(
                     out=o,
-                    lhsT=wperm[w][:, 128 * t : 128 * t + 128].bitcast(FP8X4),
-                    lhsT_scale=sperm[w[0]][k:128, 128 * t : 128 * t + 128],
-                    rhs=xc[b, v][:, c0:c1].bitcast(FP8X4),
-                    rhs_scale=xs[b, v][:, c0:c1],
+                    lhsT=wperm[n[0]][:, PART[w], 128 * t : 128 * t + 128].bitcast(FP8X4),
+                    lhsT_scale=sperm[n[0]][4 * PART[w] : 128, 128 * t : 128 * t + 128],
+                    rhs=xpart(xc, b, v, c0, c1).bitcast(FP8X4),
+                    rhs_scale=xpart(xs, b, v, c0, c1),
                     start=(i == 0),
                     stop=(i == 1),
                 )
 
-        def mm_v(b, n, j):
+        def tile_v(b, n, j):
             bank = psum.tile([P, 4, 128], F32, name="bank")
             for t in range(4):
                 project(bank[:, t, :], b, n, t, 128 * j, 128 * j + 128)
-            return bank
-
-        def evac_v(b, n, j, bank):
             nc.vector.tensor_tensor(
-                out=yg[b, n][:, 128 * j : 128 * j + 128, :],
+                out=yg[b, n[0]][:, PART[n[2:]], 128 * j : 128 * j + 128, :],
                 in0=bank[:].rearrange("p t c -> p c t"),
                 in1=bias[n][:].unsqueeze(1).to_broadcast([P, 128, 4]),
                 op=ADD,
             )
 
-        def mm_s(b, n, t):
+        def evac_s(b, n, t, c0, c1, src):
+            nc.scalar.activation(out=yst[b, n][:, t // 2, c0:c1, t % 2], in_=src, func=IDENT, bias=bias[n][:, t : t + 1], scale=1.0)
+
+        def tile_s(b, n, t):
             bank = psum.tile([P, S], F32, name="bank")
             project(bank[:], b, n, t, 0, S)
-            return bank
+            evac_s(b, n, t, 0, S, bank[:])
 
-        def mm_s_half(b, n, h, tt):
+        def half_s(b, n, h, tt):
             bank = psum.tile([P, 2, 256], F32, name="bank")
             for i in range(2):
                 project(bank[:, i, :], b, n, 2 * tt + i, 256 * h, 256 * h + 256)
-            return bank
+            for i in range(2):
+                evac_s(b, n, 2 * tt + i, 256 * h, 256 * h + 256, bank[:, i, :])
 
-        def evac_s(b, n, t, c0, c1, src):
-            nc.scalar.activation(
-                out=yst[b, n][:, t, c0:c1], in_=src, func=IDENT, bias=bias[n][:, t : t + 1], scale=1.0
-            )
-
-        def interleave_s(b, n, c0, c1):
-            nc.scalar.copy(
-                out=yg[b, n][:, c0:c1, :].rearrange("p (c i) t -> p c t i", i=4),
-                in_=yst[b, n][:, :, c0:c1].rearrange("p t (c i) -> p c t i", i=4),
-            )
-
-        def interleave_g(b, n, c0, c1):
-            for c in range(c0, c1, 128):
-                nc.gpsimd.tensor_scalar(
-                    out=yg[b, n][:, c : c + 128, :],
-                    in0=yst[b, n][:, :, c : c + 128].rearrange("p t c -> p c t"),
-                    scalar1=1.0, scalar2=0.0, op0=MULT, op1=ADD,
-                )
+        def interleave(b, n, c0, c1, eng):
+            o = yg[b, n[0]][:, PART[n[2:]], c0:c1, :].rearrange("p c t -> p (c t)").bitcast(F32).rearrange("p (c w) -> p c w", w=2)
+            i = yst[b, n][:, :, c0:c1, :].rearrange("p w c e -> p w (c e)").bitcast(F32).rearrange("p w c -> p c w")
+            if eng == "v":
+                nc.vector.tensor_copy(out=o, in_=i)
+            else:
+                nc.scalar.copy(out=o, in_=i)
 
         def score(b, j, eng):
-            banks = 1 if len(eng) == 1 else 2
-            w = S // banks
-            for i in range(banks):
+            w = S // len(eng)
+            for i in range(len(eng)):
                 bank = psum.tile([P, w], F32, name="bank")
-                for k, v in enumerate(("im", "re")):
+                for k in range(2):
                     nc.tensor.matmul_mx(
                         out=bank[:],
-                        lhsT=yc[b, "q_" + v][:, 128 * j : 128 * j + 128].bitcast(FP8X4),
-                        lhsT_scale=ys[b, "q_" + v][:, 128 * j : 128 * j + 128],
-                        rhs=yc[b, "k_" + v][:, w * i : w * i + w].bitcast(FP8X4),
-                        rhs_scale=ys[b, "k_" + v][:, w * i : w * i + w],
+                        lhsT=yc[b, "q"][:, k, 128 * j : 128 * j + 128].bitcast(FP8X4),
+                        lhsT_scale=ys[b, "q"][:, k, 128 * j : 128 * j + 128],
+                        rhs=yc[b, "k"][:, k, w * i : w * i + w].bitcast(FP8X4),
+                        rhs_scale=ys[b, "k"][:, k, w * i : w * i + w],
                         start=(k == 0),
                         stop=(k == 1),
                     )
@@ -313,118 +278,85 @@ def tile_teleportationattention_pa_w8_kernel(
                     in_=ot[b][:, j, w * i : w * i + w],
                 )
 
-        def interleave_v(b, n, c0, c1):
-            nc.vector.tensor_copy(
-                out=yg[b, n][:, c0:c1, :],
-                in_=yst[b, n][:, :, c0:c1].rearrange("p t c -> p c t"),
-            )
-
-        def cast_all(b):
-            nc.vector.tensor_copy(
-                out=xrb[b][:].rearrange("p j k -> p (j k)"),
-                in_=x8[b][:].rearrange("p j k -> p (j k)").bitcast(FP8),
-            )
-
-        cast(0, 0, "v")
-        cast(0, 1, "s")
-        cast(0, 2, "v")
-        cast(0, 3, "s")
+        cast(0, 0, 1, "v")
+        cast(0, 1, 2, "s")
+        cast(0, 2, 3, "v")
+        cast(0, 3, 4, "s")
+        cast(1, 0, 4, "v")
         warm_up(5)
-        tr = {}
-        ti = {}
-        for j in range(4):
-            tr[j] = transposes_r(0, j)
-            if j == 1:
-                ti[0, 0] = transposes(xib[0], 0)
-        evac_r1(0, 0, tr[0])
-        evac_r1(0, 1, tr[1])
-        evac_i(0, 0, ti[0, 0], "s")
-        permute_words("q_re", nc.vector)
-        quant_x(0, "r", 0, 256)
-        permute_words("q_im", nc.vector)
-        quant_x(0, "i", 0, 256)
-        permute_scales("q", nc.vector)
-        negate(0, 0, 256)
+        tr0 = transposes(xrb[0], 0, 1)
+        tr1 = transposes(xrb[0], 1, 1)
+        ti0 = transposes(xib[0], 0, 2)
+        tr2 = transposes(xrb[0], 2, 2)
+        ti1 = transposes(xib[0], 2, 2)
+        tr4 = transposes(xrb[1], 0, 2)
+        tr5 = transposes(xrb[1], 2, 2)
+        evac_i(0, 0, 2, ti0)
+        evac_i(0, 2, 2, ti1)
+        negate(0, 0, 256, "s")
+        evac_r(0, 0, 1, tr0)
+        evac_r(0, 1, 1, tr1)
+        evac_r(0, 2, 2, tr2)
+        permute_words("q", 1, 2)
+        quant_x(0, 1, 2, 0, 256)
+        permute_words("q", 0, 1)
+        permute_scales("q")
+        quant_x(0, 0, 1, 0, 256)
+        ti2 = transposes(xib[1], 0, 2)
+        ti3 = transposes(xib[1], 2, 2)
+        evac_i(1, 0, 2, ti2)
+        evac_i(1, 2, 2, ti3)
         warm_up(3)
-
-        def half_s(b, n, h, tt):
-            bank = mm_s_half(b, n, h, tt)
-            for i in range(2):
-                evac_s(b, n, 2 * tt + i, 256 * h, 256 * h + 256, bank[:, i, :])
-
-        def tile_v(b, n, j):
-            evac_v(b, n, j, mm_v(b, n, j))
-
-        def tile_s(b, n, t):
-            bank = mm_s(b, n, t)
-            evac_s(b, n, t, 0, S, bank[:])
-
         half_s(0, "q_im", 0, 0)
         half_s(0, "q_im", 0, 1)
-        quant_x(0, "n", 0, 256)
-        evac_r1(0, 2, tr[2])
-        evac_r1(0, 3, tr[3])
-        ti[0, 1] = transposes(xib[0], 1)
-        evac_i(0, 1, ti[0, 1], "s")
+        quant_x(0, 2, 3, 0, 256)
         half_s(0, "q_re", 0, 0)
         half_s(0, "q_re", 0, 1)
-        quant_x(0, "r", 256, 512)
-        quant_x(0, "i", 256, 512)
-        negate(0, 256, 512)
-        cast_all(1)
-        quant_x(0, "n", 256, 512)
+        quant_x(0, 0, 1, 256, 512)
+        quant_x(0, 1, 2, 256, 512)
+        negate(0, 256, 512, "v")
         half_s(0, "q_im", 1, 0)
         half_s(0, "q_im", 1, 1)
-        for h in range(2):
-            ti[1, h] = transposes(xib[1], h)
-            evac_i(1, h, ti[1, h], "s")
+        quant_x(0, 2, 3, 256, 512)
         half_s(0, "q_re", 1, 0)
         half_s(0, "q_re", 1, 1)
-        tr4 = transposes(xrb[1], 0)
-        tr5 = transposes(xrb[1], 1)
-        permute_words("k_re", nc.vector)
-        permute_words("k_im", nc.vector)
-        permute_scales("k", nc.vector)
-        evac_r(1, 0, tr4)
-        evac_r(1, 1, tr5)
-        interleave_g(0, "q_im", 0, 512)
+        permute_words("k", 0, 2)
+        evac_r(1, 0, 2, tr4)
+        permute_scales("k")
+        evac_r(1, 2, 2, tr5)
+        negate(1, 0, 512, "v")
+        quant_x(1, 0, 2, 0, 512)
         for j in range(4):
+            tile_v(0, "k_re", j)
             tile_s(0, "k_im", j)
-        quant_x(1, "i", 0, 512)
-        negate(1, 0, 512)
-        quant_x(1, "r", 0, 512)
-        for j in range(4):
-            tile_s(0, "k_re", j)
-        quant_x(1, "n", 0, 512)
-        interleave_g(0, "k_im", 0, 512)
-        interleave_g(0, "k_re", 0, 512)
-        quant_y(0, "q_im", 0, 512)
+            if j == 1:
+                quant_x(1, 2, 3, 0, 512)
+            if j == 1:
+                interleave(0, "q_im", 0, 512, "s")
+        interleave(0, "q_re", 0, 512, "s")
+        interleave(0, "k_im", 0, 512, "s")
         for j in range(4):
             tile_v(1, "q_im", j)
+            tile_v(1, "k_re", j)
             tile_s(1, "k_im", j)
-            interleave_s(0, "q_re", 128 * j, 128 * j + 128)
-            if j == 2:
-                quant_y(0, "k_im", 0, 512)
-        quant_y(0, "k_re", 0, 512)
-        interleave_g(1, "k_im", 0, 512)
-        for j in range(4):
             if j == 0:
-                tile_s(1, "k_re", 0)
-            if j < 3:
-                tile_s(1, "k_re", j + 1)
+                quant_y(0, "k", 1, 2, 0, 512)
+            if j == 2:
+                quant_y(0, "q", 0, 2, 0, 512)
             if j == 3:
-                interleave_s(1, "k_re", 0, 256)
-                interleave_v(1, "k_re", 256, 512)
+                quant_y(0, "k", 0, 1, 0, 512)
+        interleave(1, "k_im", 0, 512, "s")
+        for j in range(4):
             tile_v(1, "q_re", j)
             if j == 0:
-                quant_y(0, "q_re", 0, 512)
+                quant_y(1, "q", 0, 1, 0, 512)
             if j == 1:
-                quant_y(1, "q_im", 0, 512)
+                quant_y(1, "k", 1, 2, 0, 512)
             if j == 2:
-                quant_y(1, "k_im", 0, 512)
-        quant_y(1, "k_re", 0, 512)
-        quant_y(1, "q_re", 0, 512)
-        for j in range(4):
+                quant_y(1, "k", 0, 1, 0, 512)
+            if j > 0:
+                quant_y(1, "q", 1, 2, 128 * j - 128, 128 * j)
             score(0, j, "s")
+        quant_y(1, "q", 1, 2, 384, 512)
         for j in range(4):
-            score(1, j, ("v", "s", "v", "sv")[j])
+            score(1, j, ("s", "v", "s", "vs")[j])

@@ -6,6 +6,8 @@ from concourse.masks import make_identity
 B, S, D, E = 2, 512, 512, 512
 P = 128
 J = 4
+T = 4
+TOKENS = ("(p j) k -> p j k", "(j p) k -> p j k")
 
 F32 = mybir.dt.float32
 BF16 = mybir.dt.bfloat16
@@ -17,14 +19,13 @@ FP8X4 = mybir.dt.float8_e4m3fn_x4
 ADD = mybir.AluOpType.add
 MULT = mybir.AluOpType.mult
 COPY = mybir.ActivationFunctionType.Copy
-IDENT = mybir.ActivationFunctionType.Identity
-
-TOKENS = ("(p j) k -> p j k", "(j p) k -> p j k")
+IDENTITY = mybir.ActivationFunctionType.Identity
 
 FLOPS = 8 * 2 * B * S * D * E + 2 * 2 * B * S * S * E
 
-XSLOT = {"r": 0, "i": 1, "n": 2}
-HALVES = (1, 1)
+X_RE, X_IM, X_NEG = 0, 1, 2
+IM, RE = 0, 1
+PASSES = {IM: ((X_IM, RE), (X_RE, IM)), RE: ((X_RE, RE), (X_NEG, IM))}
 
 
 def tile_teleportationattention_pa_w8_kernel(
@@ -38,325 +39,291 @@ def tile_teleportationattention_pa_w8_kernel(
         psum = ctx.enter_context(tc.psum_pool(name="psum", bufs=8))
         ctx.enter_context(tc.manual_schedule())
 
-        def sb(shape, dtype, name):
+        def sbuf(shape, dtype, name):
             return keep.tile(shape, dtype, name=name, align_bytes=64)
 
-        x8 = [sb([P, J, D], U8, "x8_%d" % b) for b in range(B)]
-        xrb = [sb([P, J, D], BF16, "xrb_%d" % b) for b in range(B)]
-        xib = [sb([P, J, D], BF16, "xib_%d" % b) for b in range(B)]
-        xg = [sb([P, HALVES[b], 3, S // HALVES[b], 4], BF16, "xg_%d" % b) for b in range(B)]
-        xc = [sb([P, HALVES[b], 3, S // HALVES[b]], U32, "xc_%d" % b) for b in range(B)]
-        xs = [sb([P, HALVES[b], 3, S // HALVES[b]], U8, "xs_%d" % b) for b in range(B)]
-        scol = sb([P, 4], F32, "scol")
-        wraw = {}
-        wperm = {}
-        sraw = {}
-        sperm = {}
-        for n in ("q", "k"):
-            wraw[n] = sb([P, 2, E], I32, "wraw_" + n)
-            wperm[n] = sb([P, 2, E], I32, "wperm_" + n)
-            sraw[n] = sb([P, E], U8, "sraw_" + n)
-            sperm[n] = sb([P, E], U8, "sperm_" + n)
-        PART = {"im": 0, "re": 1}
-        bias = {}
-        for n in ("q_re", "q_im", "k_re", "k_im"):
-            bias[n] = sb([P, 4], BF16, "bias_" + n)
-        yg = {}
-        yc = {}
-        ys = {}
-        for b in range(B):
-            for n in ("q", "k"):
-                yg[b, n] = sb([P, 2, S, 4], BF16, "yg_%d%s" % (b, n))
-                yc[b, n] = sb([P, 2, S], U32, "yc_%d%s" % (b, n))
-                ys[b, n] = sb([P, 2, S], U8, "ys_%d%s" % (b, n))
-        yst = {}
-        for b, n in ((0, "q_im"), (0, "q_re"), (0, "k_im"), (1, "k_im")):
-            yst[b, n] = sb([P, 2, S, 2], BF16, "yst_%d%s" % (b, n))
-        ot = [sb([P, J, S], F32, "ot_%d" % b) for b in range(B)]
-        ident = sb([P, P], F32, "ident")
-        warm = sb([P, 16], F32, "warm")
-        wz = sb([P, 512], BF16, "wz")
+        def bank(shape, dtype=F32):
+            return psum.tile(shape, dtype, name="bank")
 
-        words = {"q_re": wq_re_words, "q_im": wq_im_words, "k_re": wk_re_words, "k_im": wk_im_words}
-        wscales = {"q_re": wq_re_scales, "q_im": wq_im_scales, "k_re": wk_re_scales, "k_im": wk_im_scales}
-        biases = {"q_re": bq_re, "q_im": bq_im, "k_re": bk_re, "k_im": bk_im}
+        x_bytes = [sbuf([P, J, D], U8, "x_bytes_%d" % b) for b in range(B)]
+        x_re_rows = [sbuf([P, J, D], BF16, "x_re_rows_%d" % b) for b in range(B)]
+        x_im_rows = [sbuf([P, J, D], BF16, "x_im_rows_%d" % b) for b in range(B)]
+        x_grouped = [sbuf([P, 3, S, T], BF16, "x_grouped_%d" % b) for b in range(B)]
+        x_words = [sbuf([P, 3, S], U32, "x_words_%d" % b) for b in range(B)]
+        x_planes = [sbuf([P, 3, S], U8, "x_planes_%d" % b) for b in range(B)]
+        x_scale = sbuf([P, T], F32, "x_scale")
 
-        nc.vector.memset(sraw["q"][:].bitcast(I32), 0)
-        nc.vector.memset(wz[:], 0.0)
-        nc.vector.memset(sraw["k"][:].bitcast(I32), 0)
-        nc.vector.memset(warm[:], 0.0)
+        w_loaded = {m: sbuf([P, 2, E], I32, "w_loaded_" + m) for m in "qk"}
+        w_words = {m: sbuf([P, 2, E], I32, "w_words_" + m) for m in "qk"}
+        w_planes_loaded = {m: sbuf([P, E], U8, "w_planes_loaded_" + m) for m in "qk"}
+        w_planes = {m: sbuf([P, E], U8, "w_planes_" + m) for m in "qk"}
+        bias = {(m, w): sbuf([P, T], BF16, "bias_%s%d" % (m, w)) for m in "qk" for w in (IM, RE)}
 
-        def load_words(n):
-            nc.sync.dma_start(out=wraw[n[0]][:, PART[n[2:]], :], in_=words[n][0].rearrange("p n t -> p (n t)").bitcast(I32))
+        y_grouped = {(b, m): sbuf([P, 2, S, T], BF16, "y_grouped_%d%s" % (b, m)) for b in range(B) for m in "qk"}
+        y_words = {(b, m): sbuf([P, 2, S], U32, "y_words_%d%s" % (b, m)) for b in range(B) for m in "qk"}
+        y_planes = {(b, m): sbuf([P, 2, S], U8, "y_planes_%d%s" % (b, m)) for b in range(B) for m in "qk"}
+        scalar_units = ((0, "q", IM), (0, "q", RE), (0, "k", IM), (1, "k", IM))
+        y_pairs = {u: sbuf([P, 2, S, 2], BF16, "y_pairs_%d%s%d" % u) for u in scalar_units}
+        scores = [sbuf([P, J, S], F32, "scores_%d" % b) for b in range(B)]
 
-        def load_scales(n):
-            k = 4 * PART[n[2:]]
+        identity = sbuf([P, P], F32, "identity")
+        table = sbuf([P, 16], F32, "table")
+        zeros = sbuf([P, 512], BF16, "zeros")
+
+        words = {("q", RE): wq_re_words, ("q", IM): wq_im_words, ("k", RE): wk_re_words, ("k", IM): wk_im_words}
+        scales = {("q", RE): wq_re_scales, ("q", IM): wq_im_scales, ("k", RE): wk_re_scales, ("k", IM): wk_im_scales}
+        biases = {("q", RE): bq_re, ("q", IM): bq_im, ("k", RE): bk_re, ("k", IM): bk_im}
+
+        nc.vector.memset(w_planes_loaded["q"][:].bitcast(I32), 0)
+        nc.vector.memset(zeros[:], 0.0)
+        nc.vector.memset(w_planes_loaded["k"][:].bitcast(I32), 0)
+        nc.vector.memset(table[:], 0.0)
+
+        def load_x_re(b, j0, j1):
+            nc.sync.dma_start(out=x_bytes[b][:, j0:j1, :], in_=x_re_bytes[b].rearrange(TOKENS[b], j=J)[:, j0:j1, :])
+
+        def load_x_im(b):
+            nc.sync.dma_start(out=x_im_rows[b][:], in_=x_im[b].rearrange(TOKENS[b], j=J))
+
+        def load_words(m, w):
+            nc.sync.dma_start(out=w_loaded[m][:, w, :], in_=words[m, w][0].rearrange("p n t -> p (n t)").bitcast(I32))
+
+        def load_scales(m, w):
             for q in range(4):
+                p0 = 32 * q + 4 * w
                 nc.sync.dma_start(
-                    out=sraw[n[0]][32 * q + k : 32 * q + k + 4, :].bitcast(I32),
-                    in_=wscales[n][0, 4 * q : 4 * q + 4, :].bitcast(I32),
+                    out=w_planes_loaded[m][p0 : p0 + 4, :].bitcast(I32),
+                    in_=scales[m, w][0, 4 * q : 4 * q + 4, :].bitcast(I32),
                 )
 
-        def load_x(b):
-            nc.sync.dma_start(out=x8[b][:], in_=x_re_bytes[b].rearrange(TOKENS[b], j=J))
+        def load_bias(m, w):
+            nc.gpsimd.dma_start(out=bias[m, w][:], in_=biases[m, w].rearrange("(p t) -> p t", t=T))
 
-        def load_xi(eng, b, h0, h1):
-            eng.dma_start(out=xib[b][:, 2 * h0 : 2 * h1, :], in_=x_im[b].rearrange(TOKENS[b], j=J)[:, 2 * h0 : 2 * h1, :])
+        nc.gpsimd.dma_start(out=x_scale[:], in_=x_re_scale.rearrange("a b (p t) -> p (a b t)", t=T))
+        make_identity(nc, identity[:])
+        load_x_re(0, 0, 2)
+        load_x_re(0, 2, 4)
+        load_x_re(1, 0, 4)
+        load_scales("q", RE)
+        load_x_im(0)
+        load_words("q", RE)
+        load_x_im(1)
+        load_words("q", IM)
+        load_scales("q", IM)
+        for m in "qk":
+            for w in ((IM, RE) if m == "q" else (RE, IM)):
+                load_bias(m, w)
+        load_words("k", RE)
+        load_words("k", IM)
+        load_scales("k", RE)
+        load_scales("k", IM)
 
-        def load_bias(n):
-            nc.gpsimd.dma_start(out=bias[n][:], in_=biases[n].rearrange("(p t) -> p t", t=4))
-
-        nc.gpsimd.dma_start(out=scol[:], in_=x_re_scale.rearrange("a b (p t) -> p (a b t)", t=4))
-        make_identity(nc, ident[:])
-        load_x(0)
-        load_scales("q_re")
-        load_x(1)
-        load_xi(nc.sync, 0, 0, 1)
-        load_xi(nc.sync, 0, 1, 2)
-        load_xi(nc.sync, 1, 0, 1)
-        load_words("q_re")
-        load_words("q_im")
-        load_scales("q_im")
-        load_xi(nc.sync, 1, 1, 2)
-        load_bias("q_im")
-        load_bias("q_re")
-        load_bias("k_re")
-        load_bias("k_im")
-        load_words("k_re")
-        load_words("k_im")
-        load_scales("k_re")
-        load_scales("k_im")
-
-        def warm_up(n):
-            bank = psum.tile([P, 512], F32, name="bank")
+        def keep_warm(n):
+            idle = bank([P, 512])
             for i in range(n):
-                nc.tensor.matmul(bank[:], lhsT=wz[:, 0:128], rhs=wz[:], start=True, stop=True)
+                nc.tensor.matmul(idle[:], lhsT=zeros[:, 0:P], rhs=zeros[:], start=True, stop=True)
 
-        nc.scalar.activation(out=warm[:], in_=warm[:], func=IDENT, bias=warm[:, 0:1], scale=1.0)
-
-        def permute_words(n, a, z):
-            nc.vector.tensor_copy(
-                out=wperm[n][:, a:z, :].rearrange("p w (t m) -> p w t m", t=4),
-                in_=wraw[n][:, a:z, :].rearrange("p w (m t) -> p w t m", t=4),
-            )
-
-        def permute_scales(n):
-            nc.vector.tensor_copy(
-                out=sperm[n][:].rearrange("p (t m) -> p t m", t=4),
-                in_=sraw[n][:].rearrange("p (m t) -> p t m", t=4),
-            )
-
-        def cast(b, j0, j1, eng):
-            src = x8[b][:, j0:j1, :].bitcast(FP8)
-            if eng == "v":
-                nc.vector.tensor_copy(out=xrb[b][:, j0:j1, :], in_=src)
+        def cast(b, j0, j1, engine):
+            source = x_bytes[b][:, j0:j1, :].bitcast(FP8)
+            if engine == "vector":
+                nc.vector.tensor_copy(out=x_re_rows[b][:, j0:j1, :], in_=source)
             else:
-                nc.scalar.copy(out=xrb[b][:, j0:j1, :], in_=src)
+                nc.scalar.copy(out=x_re_rows[b][:, j0:j1, :], in_=source)
 
-        def xpart(t, b, v, c0, c1):
-            n = S // HALVES[b]
-            h = c0 // n
-            return t[b][:, h, XSLOT[v], c0 - h * n : c1 - h * n]
-
-        def transposes(src, j0, n):
-            bank = psum.tile([P, 2, 128 * n], F32, name="bank")
-            for jj in range(n):
-                w = src[:, j0 + jj, :].bitcast(F32)
+        def transpose(rows, j0):
+            turned = bank([P, 2, 256])
+            for j in range(2):
+                pairs = rows[:, j0 + j, :].bitcast(F32)
                 for u in range(2):
-                    nc.tensor.transpose(bank[:, u, 128 * jj : 128 * jj + 128], w[:, u:256:2], ident[:])
-            return bank
+                    nc.tensor.transpose(turned[:, u, P * j : P * j + P], pairs[:, u : D // 2 : 2], identity[:])
+            return turned
 
-        def evac_r(b, j0, n, bank):
+        def group_x_re(b, j0, turned):
             nc.vector.tensor_tensor(
-                out=xpart(xg, b, "r", 128 * j0, 128 * (j0 + n)).rearrange("p c (u e) -> p c u e", e=2),
-                in0=bank[:].rearrange("p u c -> p (u c)").bitcast(BF16).rearrange("p (u c e) -> p c u e", u=2, e=2),
-                in1=scol[:].rearrange("p (u e) -> p u e", e=2).unsqueeze(1).to_broadcast([P, 128 * n, 2, 2]),
+                out=x_grouped[b][:, X_RE, P * j0 : P * j0 + 256, :].rearrange("p c (u e) -> p c u e", e=2),
+                in0=turned[:].rearrange("p u c -> p (u c)").bitcast(BF16).rearrange("p (u c e) -> p c u e", u=2, e=2),
+                in1=x_scale[:].rearrange("p (u e) -> p u e", e=2).unsqueeze(1).to_broadcast([P, 256, 2, 2]),
                 op=MULT,
             )
 
-        def evac_i(b, j0, n, bank):
-            nc.scalar.copy(
-                out=xpart(xg, b, "i", 128 * j0, 128 * (j0 + n)).rearrange("p c t -> p (c t)").bitcast(F32).rearrange("p (c u) -> p c u", u=2),
-                in_=bank[:].rearrange("p u c -> p c u"),
-            )
+        def group_x_im(b, j0, turned):
+            grouped = x_grouped[b][:, X_IM, P * j0 : P * j0 + 256, :].rearrange("p c t -> p (c t)").bitcast(F32)
+            nc.scalar.copy(out=grouped.rearrange("p (c u) -> p c u", u=2), in_=turned[:].rearrange("p u c -> p c u"))
 
-        def negate(b, c0, c1, eng):
-            o = xg[b][:, 0, 2, c0:c1].rearrange("p c t -> p (c t)")
-            i = xg[b][:, 0, 1, c0:c1].rearrange("p c t -> p (c t)")
-            if eng == "v":
-                nc.vector.tensor_scalar(out=o, in0=i, scalar1=-1.0, scalar2=None, op0=MULT)
+        def negate(b, c0, c1, engine):
+            source = x_grouped[b][:, X_IM, c0:c1, :].rearrange("p c t -> p (c t)")
+            negated = x_grouped[b][:, X_NEG, c0:c1, :].rearrange("p c t -> p (c t)")
+            if engine == "vector":
+                nc.vector.tensor_scalar(out=negated, in0=source, scalar1=-1.0, scalar2=None, op0=MULT)
             else:
-                nc.scalar.activation(out=o, in_=i, func=COPY, scale=-1.0)
+                nc.scalar.activation(out=negated, in_=source, func=COPY, scale=-1.0)
 
-        def quant_x(b, a, z, c0, c1):
-            assert z - a == 1 or c1 - c0 == S
+        def quantise(words_out, planes_out, grouped, parts, c0=0, c1=S):
             nc.vector.quantize_mx(
-                out=xc[b][:, 0, a:z, c0:c1].rearrange("p v c -> p (v c)").bitcast(FP8X4),
-                scales=xs[b][:, 0, a:z, c0:c1].rearrange("p v c -> p (v c)"),
-                in_=xg[b][:, 0, a:z, c0:c1].rearrange("p v c t -> p (v c t)"),
+                out=words_out[:, parts, c0:c1].rearrange("p v c -> p (v c)").bitcast(FP8X4),
+                scales=planes_out[:, parts, c0:c1].rearrange("p v c -> p (v c)"),
+                in_=grouped[:, parts, c0:c1, :].rearrange("p v c t -> p (v c t)"),
             )
 
-        def quant_y(b, n, a, z, c0, c1):
-            nc.vector.quantize_mx(
-                out=yc[b, n][:, a:z, c0:c1].rearrange("p v c -> p (v c)").bitcast(FP8X4),
-                scales=ys[b, n][:, a:z, c0:c1].rearrange("p v c -> p (v c)"),
-                in_=yg[b, n][:, a:z, c0:c1, :].rearrange("p v c t -> p (v c t)"),
+        def quantise_x(b, first, last):
+            quantise(x_words[b], x_planes[b], x_grouped[b], slice(first, last + 1))
+
+        def quantise_y(b, m, first, last, c0=0, c1=S):
+            quantise(y_words[b, m], y_planes[b, m], y_grouped[b, m], slice(first, last + 1), c0, c1)
+
+        def move_words(m, first, last):
+            nc.vector.tensor_copy(
+                out=w_words[m][:, first : last + 1, :].rearrange("p w (t i) -> p w t i", t=T),
+                in_=w_loaded[m][:, first : last + 1, :].rearrange("p w (i t) -> p w t i", t=T),
             )
 
-        def project(o, b, n, t, c0, c1):
-            for i, (v, w) in enumerate(((("i", "re"), ("r", "im")) if n[2:] == "im" else (("r", "re"), ("n", "im")))):
+        def move_scales(m):
+            nc.vector.tensor_copy(
+                out=w_planes[m][:].rearrange("p (t i) -> p t i", t=T),
+                in_=w_planes_loaded[m][:].rearrange("p (i t) -> p t i", t=T),
+            )
+
+        def project(sums, b, m, w, t, c0, c1):
+            for n, (xv, wv) in enumerate(PASSES[w]):
                 nc.tensor.matmul_mx(
-                    out=o,
-                    lhsT=wperm[n[0]][:, PART[w], 128 * t : 128 * t + 128].bitcast(FP8X4),
-                    lhsT_scale=sperm[n[0]][4 * PART[w] : 128, 128 * t : 128 * t + 128],
-                    rhs=xpart(xc, b, v, c0, c1).bitcast(FP8X4),
-                    rhs_scale=xpart(xs, b, v, c0, c1),
-                    start=(i == 0),
-                    stop=(i == 1),
+                    out=sums,
+                    lhsT=w_words[m][:, wv, P * t : P * t + P].bitcast(FP8X4),
+                    lhsT_scale=w_planes[m][4 * wv : P, P * t : P * t + P],
+                    rhs=x_words[b][:, xv, c0:c1].bitcast(FP8X4),
+                    rhs_scale=x_planes[b][:, xv, c0:c1],
+                    start=(n == 0),
+                    stop=(n == 1),
                 )
 
-        def tile_v(b, n, j):
-            bank = psum.tile([P, 4, 128], F32, name="bank")
-            for t in range(4):
-                project(bank[:, t, :], b, n, t, 128 * j, 128 * j + 128)
+        def project_on_vector(b, m, w, j):
+            sums = bank([P, T, P])
+            for t in range(T):
+                project(sums[:, t, :], b, m, w, t, P * j, P * j + P)
             nc.vector.tensor_tensor(
-                out=yg[b, n[0]][:, PART[n[2:]], 128 * j : 128 * j + 128, :],
-                in0=bank[:].rearrange("p t c -> p c t"),
-                in1=bias[n][:].unsqueeze(1).to_broadcast([P, 128, 4]),
+                out=y_grouped[b, m][:, w, P * j : P * j + P, :],
+                in0=sums[:].rearrange("p t c -> p c t"),
+                in1=bias[m, w][:].unsqueeze(1).to_broadcast([P, P, T]),
                 op=ADD,
             )
 
-        def evac_s(b, n, t, c0, c1, src):
-            nc.scalar.activation(out=yst[b, n][:, t // 2, c0:c1, t % 2], in_=src, func=IDENT, bias=bias[n][:, t : t + 1], scale=1.0)
+        def project_on_scalar(b, m, w, t):
+            sums = bank([P, S])
+            project(sums[:], b, m, w, t, 0, S)
+            nc.scalar.activation(
+                out=y_pairs[b, m, w][:, t // 2, :, t % 2],
+                in_=sums[:],
+                func=IDENTITY,
+                bias=bias[m, w][:, t : t + 1],
+                scale=1.0,
+            )
 
-        def tile_s(b, n, t):
-            bank = psum.tile([P, S], F32, name="bank")
-            project(bank[:], b, n, t, 0, S)
-            evac_s(b, n, t, 0, S, bank[:])
-
-        def half_s(b, n, h, tt):
-            bank = psum.tile([P, 2, 256], F32, name="bank")
-            for i in range(2):
-                project(bank[:, i, :], b, n, 2 * tt + i, 256 * h, 256 * h + 256)
-            for i in range(2):
-                evac_s(b, n, 2 * tt + i, 256 * h, 256 * h + 256, bank[:, i, :])
-
-        def interleave(b, n, c0, c1, eng):
-            o = yg[b, n[0]][:, PART[n[2:]], c0:c1, :].rearrange("p c t -> p (c t)").bitcast(F32).rearrange("p (c w) -> p c w", w=2)
-            i = yst[b, n][:, :, c0:c1, :].rearrange("p w c e -> p w (c e)").bitcast(F32).rearrange("p w c -> p c w")
-            if eng == "v":
-                nc.vector.tensor_copy(out=o, in_=i)
+        def group_pairs(b, m, w, engine):
+            grouped = y_grouped[b, m][:, w, :, :].rearrange("p c t -> p (c t)").bitcast(F32).rearrange("p (c h) -> p c h", h=2)
+            pairs = y_pairs[b, m, w][:].rearrange("p h c i -> p h (c i)").bitcast(F32).rearrange("p h c -> p c h")
+            if engine == "vector":
+                nc.vector.tensor_copy(out=grouped, in_=pairs)
             else:
-                nc.scalar.copy(out=o, in_=i)
+                nc.scalar.copy(out=grouped, in_=pairs)
 
-        def score(b, j, eng):
-            w = S // len(eng)
-            for i in range(len(eng)):
-                bank = psum.tile([P, w], F32, name="bank")
-                for k in range(2):
+        def score(b, j, engines):
+            share = S // len(engines)
+            for n, engine in enumerate(engines):
+                keys = slice(share * n, share * n + share)
+                sums = bank([P, share])
+                for w in (IM, RE):
                     nc.tensor.matmul_mx(
-                        out=bank[:],
-                        lhsT=yc[b, "q"][:, k, 128 * j : 128 * j + 128].bitcast(FP8X4),
-                        lhsT_scale=ys[b, "q"][:, k, 128 * j : 128 * j + 128],
-                        rhs=yc[b, "k"][:, k, w * i : w * i + w].bitcast(FP8X4),
-                        rhs_scale=ys[b, "k"][:, k, w * i : w * i + w],
-                        start=(k == 0),
-                        stop=(k == 1),
+                        out=sums[:],
+                        lhsT=y_words[b, "q"][:, w, P * j : P * j + P].bitcast(FP8X4),
+                        lhsT_scale=y_planes[b, "q"][:, w, P * j : P * j + P],
+                        rhs=y_words[b, "k"][:, w, keys].bitcast(FP8X4),
+                        rhs_scale=y_planes[b, "k"][:, w, keys],
+                        start=(w == IM),
+                        stop=(w == RE),
                     )
                 if b == 0:
-                    o = ot[b][:, j, :].rearrange("p (c i) -> p c i", i=J)
-                    a = bank[:].rearrange("p (i c) -> p c i", i=J)
+                    stored = scores[b][:, j, :].rearrange("p (c i) -> p c i", i=J)
+                    computed = sums[:].rearrange("p (i c) -> p c i", i=J)
                 else:
-                    o = ot[b][:, j, w * i : w * i + w]
-                    a = bank[:]
-                if eng[i] == "v":
-                    nc.vector.tensor_copy(out=o, in_=a)
+                    stored = scores[b][:, j, keys]
+                    computed = sums[:]
+                if engine == "vector":
+                    nc.vector.tensor_copy(out=stored, in_=computed)
                 else:
-                    nc.scalar.copy(out=o, in_=a)
-                nc.sync.dma_start(
-                    out=out[b].rearrange(TOKENS[b], j=J)[:, j, w * i : w * i + w],
-                    in_=ot[b][:, j, w * i : w * i + w],
-                )
+                    nc.scalar.copy(out=stored, in_=computed)
+                nc.sync.dma_start(out=out[b].rearrange(TOKENS[b], j=J)[:, j, keys], in_=scores[b][:, j, keys])
 
-        cast(0, 0, 1, "v")
-        cast(0, 1, 2, "s")
-        cast(0, 2, 3, "v")
-        cast(0, 3, 4, "s")
-        cast(1, 0, 4, "v")
-        warm_up(5)
-        tr0 = transposes(xrb[0], 0, 1)
-        tr1 = transposes(xrb[0], 1, 1)
-        ti0 = transposes(xib[0], 0, 2)
-        tr2 = transposes(xrb[0], 2, 2)
-        ti1 = transposes(xib[0], 2, 2)
-        tr4 = transposes(xrb[1], 0, 2)
-        tr5 = transposes(xrb[1], 2, 2)
-        evac_i(0, 0, 2, ti0)
-        evac_i(0, 2, 2, ti1)
-        negate(0, 0, 256, "s")
-        evac_r(0, 0, 1, tr0)
-        evac_r(0, 1, 1, tr1)
-        evac_r(0, 2, 2, tr2)
-        permute_words("q", 1, 2)
-        quant_x(0, 1, 2, 0, 256)
-        permute_words("q", 0, 1)
-        permute_scales("q")
-        quant_x(0, 0, 1, 0, 256)
-        ti2 = transposes(xib[1], 0, 2)
-        ti3 = transposes(xib[1], 2, 2)
-        evac_i(1, 0, 2, ti2)
-        evac_i(1, 2, 2, ti3)
-        warm_up(3)
-        half_s(0, "q_im", 0, 0)
-        half_s(0, "q_im", 0, 1)
-        quant_x(0, 2, 3, 0, 256)
-        half_s(0, "q_re", 0, 0)
-        half_s(0, "q_re", 0, 1)
-        quant_x(0, 0, 1, 256, 512)
-        quant_x(0, 1, 2, 256, 512)
-        negate(0, 256, 512, "v")
-        half_s(0, "q_im", 1, 0)
-        half_s(0, "q_im", 1, 1)
-        quant_x(0, 2, 3, 256, 512)
-        half_s(0, "q_re", 1, 0)
-        half_s(0, "q_re", 1, 1)
-        permute_words("k", 0, 2)
-        evac_r(1, 0, 2, tr4)
-        permute_scales("k")
-        evac_r(1, 2, 2, tr5)
-        negate(1, 0, 512, "v")
-        quant_x(1, 0, 2, 0, 512)
-        for j in range(4):
-            tile_v(0, "k_re", j)
-            tile_s(0, "k_im", j)
+        nc.scalar.activation(out=table[:], in_=table[:], func=IDENTITY, bias=table[:, 0:1], scale=1.0)
+
+        cast(0, 0, 2, "vector")
+        cast(0, 2, 4, "scalar")
+        cast(1, 0, 2, "vector")
+        cast(1, 2, 4, "scalar")
+        keep_warm(5)
+        turned_re = {(0, 0): transpose(x_re_rows[0], 0), (0, 2): transpose(x_re_rows[0], 2)}
+        turned_im = {(0, 0): transpose(x_im_rows[0], 0), (0, 2): transpose(x_im_rows[0], 2)}
+        turned_re[1, 0] = transpose(x_re_rows[1], 0)
+        turned_re[1, 2] = transpose(x_re_rows[1], 2)
+        group_x_im(0, 0, turned_im[0, 0])
+        group_x_im(0, 2, turned_im[0, 2])
+        negate(0, 0, S // 2, "scalar")
+        group_x_re(0, 0, turned_re[0, 0])
+        group_x_re(0, 2, turned_re[0, 2])
+        move_words("q", RE, RE)
+        quantise_x(0, X_RE, X_IM)
+        move_words("q", IM, IM)
+        move_scales("q")
+        turned_im[1, 0] = transpose(x_im_rows[1], 0)
+        turned_im[1, 2] = transpose(x_im_rows[1], 2)
+        group_x_im(1, 0, turned_im[1, 0])
+        group_x_im(1, 2, turned_im[1, 2])
+        keep_warm(3)
+        negate(0, S // 2, S, "vector")
+        quantise_x(0, X_NEG, X_NEG)
+
+        for w in (IM, RE):
+            for t in range(T):
+                project_on_scalar(0, "q", w, t)
+        group_x_re(1, 0, turned_re[1, 0])
+        move_words("k", IM, RE)
+        group_x_re(1, 2, turned_re[1, 2])
+        move_scales("k")
+        negate(1, 0, S, "vector")
+        quantise_x(1, X_RE, X_IM)
+
+        for j in range(J):
+            project_on_vector(0, "k", RE, j)
+            project_on_scalar(0, "k", IM, j)
             if j == 1:
-                quant_x(1, 2, 3, 0, 512)
-            if j == 1:
-                interleave(0, "q_im", 0, 512, "s")
-        interleave(0, "q_re", 0, 512, "s")
-        interleave(0, "k_im", 0, 512, "s")
-        for j in range(4):
-            tile_v(1, "q_im", j)
-            tile_v(1, "k_re", j)
-            tile_s(1, "k_im", j)
+                quantise_x(1, X_NEG, X_NEG)
+                group_pairs(0, "q", IM, "vector")
+        group_pairs(0, "q", RE, "scalar")
+        group_pairs(0, "k", IM, "scalar")
+
+        for j in range(J):
+            project_on_vector(1, "q", IM, j)
+            project_on_vector(1, "k", RE, j)
+            project_on_scalar(1, "k", IM, j)
             if j == 0:
-                quant_y(0, "k", 1, 2, 0, 512)
+                quantise_y(0, "k", RE, RE)
+            if j == 1:
+                quantise_y(0, "q", IM, RE)
             if j == 2:
-                quant_y(0, "q", 0, 2, 0, 512)
+                quantise_y(0, "k", IM, IM)
+        group_pairs(1, "k", IM, "scalar")
+
+        for j in range(J):
+            project_on_vector(1, "q", RE, j)
+            if j == 0:
+                quantise_y(1, "q", IM, IM)
+            if j == 1:
+                quantise_y(1, "k", RE, RE)
+            if j == 2:
+                quantise_y(1, "k", IM, IM)
+                quantise_y(1, "q", RE, RE, 0, 2 * P)
             if j == 3:
-                quant_y(0, "k", 0, 1, 0, 512)
-        interleave(1, "k_im", 0, 512, "s")
-        for j in range(4):
-            tile_v(1, "q_re", j)
-            if j == 0:
-                quant_y(1, "q", 0, 1, 0, 512)
-            if j == 1:
-                quant_y(1, "k", 1, 2, 0, 512)
-            if j == 2:
-                quant_y(1, "k", 0, 1, 0, 512)
-            if j > 0:
-                quant_y(1, "q", 1, 2, 128 * j - 128, 128 * j)
-            score(0, j, "s")
-        quant_y(1, "q", 1, 2, 384, 512)
-        for j in range(4):
-            score(1, j, ("s", "v", "s", "vs")[j])
+                quantise_y(1, "q", RE, RE, 2 * P, 3 * P)
+            score(0, j, ("scalar",))
+        quantise_y(1, "q", RE, RE, 3 * P, 4 * P)
+
+        for j, engines in enumerate((("scalar",), ("vector",), ("scalar",), ("vector", "scalar"))):
+            score(1, j, engines)

from contextlib import ExitStack

import concourse.mybir as mybir
from concourse.masks import make_identity

B, S, D, E = 2, 512, 512, 512
P = 128
J = 4
T = 4
TOKENS = ("(p j) k -> p j k", "(j p) k -> p j k")

F32 = mybir.dt.float32
BF16 = mybir.dt.bfloat16
U32 = mybir.dt.uint32
I32 = mybir.dt.int32
U8 = mybir.dt.uint8
FP8 = mybir.dt.float8_e4m3fn
FP8X4 = mybir.dt.float8_e4m3fn_x4
ADD = mybir.AluOpType.add
MULT = mybir.AluOpType.mult
COPY = mybir.ActivationFunctionType.Copy
IDENTITY = mybir.ActivationFunctionType.Identity

FLOPS = 8 * 2 * B * S * D * E + 2 * 2 * B * S * S * E

X_RE, X_IM, X_NEG = 0, 1, 2
IM, RE = 0, 1
PASSES = {IM: ((X_IM, RE), (X_RE, IM)), RE: ((X_RE, RE), (X_NEG, IM))}


def tile_teleportationattention_pa_w8_kernel(
    tc, x_re_bytes, x_re_scale, x_im,
    wq_re_words, wq_re_scales, wq_im_words, wq_im_scales, bq_re, bq_im,
    wk_re_words, wk_re_scales, wk_im_words, wk_im_scales, bk_re, bk_im, out,
):
    nc = tc.nc
    with ExitStack() as ctx:
        keep = ctx.enter_context(tc.tile_pool(name="keep", bufs=1))
        psum = ctx.enter_context(tc.psum_pool(name="psum", bufs=8))
        ctx.enter_context(tc.manual_schedule())

        def sbuf(shape, dtype, name):
            return keep.tile(shape, dtype, name=name, align_bytes=64)

        def bank(shape, dtype=F32):
            return psum.tile(shape, dtype, name="bank")

        x_bytes = [sbuf([P, J, D], U8, "x_bytes_%d" % b) for b in range(B)]
        x_re_rows = [sbuf([P, J, D], BF16, "x_re_rows_%d" % b) for b in range(B)]
        x_im_rows = [sbuf([P, J, D], BF16, "x_im_rows_%d" % b) for b in range(B)]
        x_grouped = [sbuf([P, 3, S, T], BF16, "x_grouped_%d" % b) for b in range(B)]
        x_words = [sbuf([P, 3, S], U32, "x_words_%d" % b) for b in range(B)]
        x_planes = [sbuf([P, 3, S], U8, "x_planes_%d" % b) for b in range(B)]
        x_scale = sbuf([P, T], F32, "x_scale")

        w_loaded = {m: sbuf([P, 2, E], I32, "w_loaded_" + m) for m in "qk"}
        w_words = {m: sbuf([P, 2, E], I32, "w_words_" + m) for m in "qk"}
        w_planes_loaded = {m: sbuf([P, E], U8, "w_planes_loaded_" + m) for m in "qk"}
        w_planes = {m: sbuf([P, E], U8, "w_planes_" + m) for m in "qk"}
        bias = {(m, w): sbuf([P, T], BF16, "bias_%s%d" % (m, w)) for m in "qk" for w in (IM, RE)}

        y_grouped = {(b, m): sbuf([P, 2, S, T], BF16, "y_grouped_%d%s" % (b, m)) for b in range(B) for m in "qk"}
        y_words = {(b, m): sbuf([P, 2, S], U32, "y_words_%d%s" % (b, m)) for b in range(B) for m in "qk"}
        y_planes = {(b, m): sbuf([P, 2, S], U8, "y_planes_%d%s" % (b, m)) for b in range(B) for m in "qk"}
        scalar_units = ((0, "q", IM), (0, "q", RE), (0, "k", IM), (1, "k", IM))
        y_pairs = {u: sbuf([P, 2, S, 2], BF16, "y_pairs_%d%s%d" % u) for u in scalar_units}
        scores = [sbuf([P, J, S], F32, "scores_%d" % b) for b in range(B)]

        identity = sbuf([P, P], F32, "identity")
        table = sbuf([P, 16], F32, "table")
        zeros = sbuf([P, 512], BF16, "zeros")

        words = {("q", RE): wq_re_words, ("q", IM): wq_im_words, ("k", RE): wk_re_words, ("k", IM): wk_im_words}
        scales = {("q", RE): wq_re_scales, ("q", IM): wq_im_scales, ("k", RE): wk_re_scales, ("k", IM): wk_im_scales}
        biases = {("q", RE): bq_re, ("q", IM): bq_im, ("k", RE): bk_re, ("k", IM): bk_im}

        nc.vector.memset(w_planes_loaded["q"][:].bitcast(I32), 0)
        nc.vector.memset(zeros[:], 0.0)
        nc.vector.memset(w_planes_loaded["k"][:].bitcast(I32), 0)
        nc.vector.memset(table[:], 0.0)

        def load_x_re(b, j0, j1):
            nc.sync.dma_start(out=x_bytes[b][:, j0:j1, :], in_=x_re_bytes[b].rearrange(TOKENS[b], j=J)[:, j0:j1, :])

        def load_x_im(b):
            nc.sync.dma_start(out=x_im_rows[b][:], in_=x_im[b].rearrange(TOKENS[b], j=J))

        def load_words(m, w):
            nc.sync.dma_start(out=w_loaded[m][:, w, :], in_=words[m, w][0].rearrange("p n t -> p (n t)").bitcast(I32))

        def load_scales(m, w):
            for q in range(4):
                p0 = 32 * q + 4 * w
                nc.sync.dma_start(
                    out=w_planes_loaded[m][p0 : p0 + 4, :].bitcast(I32),
                    in_=scales[m, w][0, 4 * q : 4 * q + 4, :].bitcast(I32),
                )

        def load_bias(m, w):
            nc.gpsimd.dma_start(out=bias[m, w][:], in_=biases[m, w].rearrange("(p t) -> p t", t=T))

        nc.gpsimd.dma_start(out=x_scale[:], in_=x_re_scale.rearrange("a b (p t) -> p (a b t)", t=T))
        make_identity(nc, identity[:])
        load_x_re(0, 0, 2)
        load_x_re(0, 2, 4)
        load_x_re(1, 0, 4)
        load_scales("q", RE)
        load_x_im(0)
        load_words("q", RE)
        load_x_im(1)
        load_words("q", IM)
        load_scales("q", IM)
        for m in "qk":
            for w in ((IM, RE) if m == "q" else (RE, IM)):
                load_bias(m, w)
        load_words("k", RE)
        load_words("k", IM)
        load_scales("k", RE)
        load_scales("k", IM)

        def keep_warm(n):
            idle = bank([P, 512])
            for i in range(n):
                nc.tensor.matmul(idle[:], lhsT=zeros[:, 0:P], rhs=zeros[:], start=True, stop=True)

        def cast(b, j0, j1, engine):
            source = x_bytes[b][:, j0:j1, :].bitcast(FP8)
            if engine == "vector":
                nc.vector.tensor_copy(out=x_re_rows[b][:, j0:j1, :], in_=source)
            else:
                nc.scalar.copy(out=x_re_rows[b][:, j0:j1, :], in_=source)

        def transpose(rows, j0):
            turned = bank([P, 2, 256])
            for j in range(2):
                pairs = rows[:, j0 + j, :].bitcast(F32)
                for u in range(2):
                    nc.tensor.transpose(turned[:, u, P * j : P * j + P], pairs[:, u : D // 2 : 2], identity[:])
            return turned

        def group_x_re(b, j0, turned):
            nc.vector.tensor_tensor(
                out=x_grouped[b][:, X_RE, P * j0 : P * j0 + 256, :].rearrange("p c (u e) -> p c u e", e=2),
                in0=turned[:].rearrange("p u c -> p (u c)").bitcast(BF16).rearrange("p (u c e) -> p c u e", u=2, e=2),
                in1=x_scale[:].rearrange("p (u e) -> p u e", e=2).unsqueeze(1).to_broadcast([P, 256, 2, 2]),
                op=MULT,
            )

        def group_x_im(b, j0, turned):
            grouped = x_grouped[b][:, X_IM, P * j0 : P * j0 + 256, :].rearrange("p c t -> p (c t)").bitcast(F32)
            nc.scalar.copy(out=grouped.rearrange("p (c u) -> p c u", u=2), in_=turned[:].rearrange("p u c -> p c u"))

        def negate(b, c0, c1, engine):
            source = x_grouped[b][:, X_IM, c0:c1, :].rearrange("p c t -> p (c t)")
            negated = x_grouped[b][:, X_NEG, c0:c1, :].rearrange("p c t -> p (c t)")
            if engine == "vector":
                nc.vector.tensor_scalar(out=negated, in0=source, scalar1=-1.0, scalar2=None, op0=MULT)
            else:
                nc.scalar.activation(out=negated, in_=source, func=COPY, scale=-1.0)

        def quantise(words_out, planes_out, grouped, parts, c0=0, c1=S):
            nc.vector.quantize_mx(
                out=words_out[:, parts, c0:c1].rearrange("p v c -> p (v c)").bitcast(FP8X4),
                scales=planes_out[:, parts, c0:c1].rearrange("p v c -> p (v c)"),
                in_=grouped[:, parts, c0:c1, :].rearrange("p v c t -> p (v c t)"),
            )

        def quantise_x(b, first, last):
            quantise(x_words[b], x_planes[b], x_grouped[b], slice(first, last + 1))

        def quantise_y(b, m, first, last, c0=0, c1=S):
            quantise(y_words[b, m], y_planes[b, m], y_grouped[b, m], slice(first, last + 1), c0, c1)

        def move_words(m, first, last):
            nc.vector.tensor_copy(
                out=w_words[m][:, first : last + 1, :].rearrange("p w (t i) -> p w t i", t=T),
                in_=w_loaded[m][:, first : last + 1, :].rearrange("p w (i t) -> p w t i", t=T),
            )

        def move_scales(m):
            nc.vector.tensor_copy(
                out=w_planes[m][:].rearrange("p (t i) -> p t i", t=T),
                in_=w_planes_loaded[m][:].rearrange("p (i t) -> p t i", t=T),
            )

        def project(sums, b, m, w, t, c0, c1):
            for n, (xv, wv) in enumerate(PASSES[w]):
                nc.tensor.matmul_mx(
                    out=sums,
                    lhsT=w_words[m][:, wv, P * t : P * t + P].bitcast(FP8X4),
                    lhsT_scale=w_planes[m][4 * wv : P, P * t : P * t + P],
                    rhs=x_words[b][:, xv, c0:c1].bitcast(FP8X4),
                    rhs_scale=x_planes[b][:, xv, c0:c1],
                    start=(n == 0),
                    stop=(n == 1),
                )

        def project_on_vector(b, m, w, j):
            sums = bank([P, T, P])
            for t in range(T):
                project(sums[:, t, :], b, m, w, t, P * j, P * j + P)
            nc.vector.tensor_tensor(
                out=y_grouped[b, m][:, w, P * j : P * j + P, :],
                in0=sums[:].rearrange("p t c -> p c t"),
                in1=bias[m, w][:].unsqueeze(1).to_broadcast([P, P, T]),
                op=ADD,
            )

        def project_on_scalar(b, m, w, t):
            sums = bank([P, S])
            project(sums[:], b, m, w, t, 0, S)
            nc.scalar.activation(
                out=y_pairs[b, m, w][:, t // 2, :, t % 2],
                in_=sums[:],
                func=IDENTITY,
                bias=bias[m, w][:, t : t + 1],
                scale=1.0,
            )

        def group_pairs(b, m, w, engine):
            grouped = y_grouped[b, m][:, w, :, :].rearrange("p c t -> p (c t)").bitcast(F32).rearrange("p (c h) -> p c h", h=2)
            pairs = y_pairs[b, m, w][:].rearrange("p h c i -> p h (c i)").bitcast(F32).rearrange("p h c -> p c h")
            if engine == "vector":
                nc.vector.tensor_copy(out=grouped, in_=pairs)
            else:
                nc.scalar.copy(out=grouped, in_=pairs)

        def score(b, j, engines):
            share = S // len(engines)
            for n, engine in enumerate(engines):
                keys = slice(share * n, share * n + share)
                sums = bank([P, share])
                for w in (IM, RE):
                    nc.tensor.matmul_mx(
                        out=sums[:],
                        lhsT=y_words[b, "q"][:, w, P * j : P * j + P].bitcast(FP8X4),
                        lhsT_scale=y_planes[b, "q"][:, w, P * j : P * j + P],
                        rhs=y_words[b, "k"][:, w, keys].bitcast(FP8X4),
                        rhs_scale=y_planes[b, "k"][:, w, keys],
                        start=(w == IM),
                        stop=(w == RE),
                    )
                if b == 0:
                    stored = scores[b][:, j, :].rearrange("p (c i) -> p c i", i=J)
                    computed = sums[:].rearrange("p (i c) -> p c i", i=J)
                else:
                    stored = scores[b][:, j, keys]
                    computed = sums[:]
                if engine == "vector":
                    nc.vector.tensor_copy(out=stored, in_=computed)
                else:
                    nc.scalar.copy(out=stored, in_=computed)
                nc.sync.dma_start(out=out[b].rearrange(TOKENS[b], j=J)[:, j, keys], in_=scores[b][:, j, keys])

        nc.scalar.activation(out=table[:], in_=table[:], func=IDENTITY, bias=table[:, 0:1], scale=1.0)

        cast(0, 0, 2, "vector")
        cast(0, 2, 4, "scalar")
        cast(1, 0, 2, "vector")
        cast(1, 2, 4, "scalar")
        keep_warm(5)
        turned_re = {(0, 0): transpose(x_re_rows[0], 0), (0, 2): transpose(x_re_rows[0], 2)}
        turned_im = {(0, 0): transpose(x_im_rows[0], 0), (0, 2): transpose(x_im_rows[0], 2)}
        turned_re[1, 0] = transpose(x_re_rows[1], 0)
        turned_re[1, 2] = transpose(x_re_rows[1], 2)
        group_x_im(0, 0, turned_im[0, 0])
        group_x_im(0, 2, turned_im[0, 2])
        negate(0, 0, S // 2, "scalar")
        group_x_re(0, 0, turned_re[0, 0])
        group_x_re(0, 2, turned_re[0, 2])
        move_words("q", RE, RE)
        quantise_x(0, X_RE, X_IM)
        move_words("q", IM, IM)
        move_scales("q")
        turned_im[1, 0] = transpose(x_im_rows[1], 0)
        turned_im[1, 2] = transpose(x_im_rows[1], 2)
        group_x_im(1, 0, turned_im[1, 0])
        group_x_im(1, 2, turned_im[1, 2])
        keep_warm(3)
        negate(0, S // 2, S, "vector")
        quantise_x(0, X_NEG, X_NEG)

        for w in (IM, RE):
            for t in range(T):
                project_on_scalar(0, "q", w, t)
        group_x_re(1, 0, turned_re[1, 0])
        move_words("k", IM, RE)
        group_x_re(1, 2, turned_re[1, 2])
        move_scales("k")
        negate(1, 0, S, "vector")
        quantise_x(1, X_RE, X_IM)

        for j in range(J):
            project_on_vector(0, "k", RE, j)
            project_on_scalar(0, "k", IM, j)
            if j == 1:
                quantise_x(1, X_NEG, X_NEG)
                group_pairs(0, "q", IM, "vector")
        group_pairs(0, "q", RE, "scalar")
        group_pairs(0, "k", IM, "scalar")

        for j in range(J):
            project_on_vector(1, "q", IM, j)
            project_on_vector(1, "k", RE, j)
            project_on_scalar(1, "k", IM, j)
            if j == 0:
                quantise_y(0, "k", RE, RE)
            if j == 1:
                quantise_y(0, "q", IM, RE)
            if j == 2:
                quantise_y(0, "k", IM, IM)
        group_pairs(1, "k", IM, "scalar")

        for j in range(J):
            project_on_vector(1, "q", RE, j)
            if j == 0:
                quantise_y(1, "q", IM, IM)
            if j == 1:
                quantise_y(1, "k", RE, RE)
            if j == 2:
                quantise_y(1, "k", IM, IM)
                quantise_y(1, "q", RE, RE, 0, 2 * P)
            if j == 3:
                quantise_y(1, "q", RE, RE, 2 * P, 3 * P)
            score(0, j, ("scalar",))
        quantise_y(1, "q", RE, RE, 3 * P, 4 * P)

        for j, engines in enumerate((("scalar",), ("vector",), ("scalar",), ("vector", "scalar"))):
            score(1, j, engines)
